import numpy as np
import ml_dtypes


def mxq(x, axis, fmt="e4m3"):
    dtype, down = {"e4m3": (ml_dtypes.float8_e4m3fn, 7), "e5m2": (ml_dtypes.float8_e5m2, 14)}[fmt]
    v = np.moveaxis(np.asarray(x, np.float32).astype(ml_dtypes.bfloat16).astype(np.float64), axis, -1)
    blocks = v.reshape(v.shape[:-1] + (-1, 32))
    amax = np.abs(blocks).max(-1, keepdims=True)
    byte = np.maximum(np.where(amax > 0, np.frexp(amax)[1] - 1 + 127, 0) - down, 1)
    scale = np.exp2(byte - 127.0)
    codes = (blocks / scale).astype(np.float32).astype(dtype).astype(np.float64)
    return np.moveaxis((codes * scale).reshape(v.shape), -1, axis)


WIDE = False


def mx_kscale(k):
    if not WIDE:
        return np.ones(k)
    levels = np.array([10, -10, 5, -5, 0])
    a = np.random.permutation(np.resize(levels, k // 512 * 4)).reshape(k // 512, 4)
    idx = np.arange(k)
    return np.exp2(a[idx // 512, idx % 128 // 32])


BF16 = ml_dtypes.bfloat16


def bf(x):
    return np.asarray(x, np.float32).astype(BF16)


def f64(x):
    return np.asarray(x).astype(np.float64)


N, D, O, H, W = 4, 512, 512, 32, 32
K = D + D
P = H * W


def sigmoid(v):
    return 1.0 / (1.0 + np.exp(-v))


def spatial_gate(re, x_orig):
    a = np.exp(re)
    e = np.exp(a - a.max(1, keepdims=True))
    sm = e / e.sum(1, keepdims=True)
    s = (sm * re).sum(1, keepdims=True)
    return x_orig * s


def setup_inputs():
    t = mx_kscale(D)
    u = t / t.max()
    uc = u[None, :, None, None]
    uu = np.concatenate([u, u])
    return {"x1": bf(np.random.standard_normal((N, D, H, W)) * 0.5 * uc), "x2": bf(np.random.standard_normal((N, D, H, W)) * 0.5 * uc),
            "FE_x1": bf(np.random.standard_normal((N, D, H, W)) * 0.5 * uc), "FE_x2": bf(np.random.standard_normal((N, D, H, W)) * 0.5 * uc),
            "g1": bf(np.random.standard_normal((N, D)) * 1.2), "g2": bf(np.random.standard_normal((N, D)) * 1.2),
            "p1_w": bf(np.random.standard_normal((O, K)) / np.sqrt(K) / uu), "p1_b": bf(np.random.standard_normal(O) * 0.3),
            "p2_w": bf(np.random.standard_normal((O, K)) / np.sqrt(K) / uu), "p2_b": bf(np.random.standard_normal(O) * 0.3)}


def reference(x1, x2, FE_x1, FE_x2, g1, g2, p1_w, p1_b, p2_w, p2_b):
    a1 = f64(x1).reshape(N, D, P)
    a2 = f64(x2).reshape(N, D, P)
    re_x1 = a1 * sigmoid(f64(g1))[:, :, None] + a2
    re_x2 = a2 * sigmoid(f64(g2))[:, :, None] + a1
    fg_x1_sp = spatial_gate(re_x1, a1) + a2
    fg_x2_sp = spatial_gate(re_x2, a2) + a1
    co_x1 = fg_x1_sp + f64(FE_x1).reshape(N, D, P)
    co_x2 = fg_x2_sp + f64(FE_x2).reshape(N, D, P)
    re = np.concatenate([co_x1, co_x2], axis=1)
    rq = mxq(re, 1, "e4m3")
    po_x1 = (mxq(f64(p1_w), 1, "e4m3") @ rq) + f64(p1_b)[None, :, None]
    po_x2 = (mxq(f64(p2_w), 1, "e4m3") @ rq) + f64(p2_b)[None, :, None]
    return po_x1.reshape(N, O, H, W), po_x2.reshape(N, O, H, W)

@@ -1,0 +1,344 @@
+from contextlib import ExitStack
+
+import concourse.mybir as mybir
+from concourse.masks import make_identity
+
+F32 = mybir.dt.float32
+BF16 = mybir.dt.bfloat16
+U32 = mybir.dt.uint32
+U8 = mybir.dt.uint8
+FP8X4 = mybir.dt.float8_e4m3fn_x4
+ALU = mybir.AluOpType
+ACT = mybir.ActivationFunctionType
+AX = mybir.AxisListType
+
+FLOPS = 2 * 1024 * 1024 * 4096
+
+P = 128
+J = 4
+GW = 512
+NG = 8
+NH = 64
+L_E = 1
+L_SER = 2
+L_T = 4
+L_Z = 5
+L_Q = 6
+PLAIN_J = 3
+V_EV = (3, 7)
+LAST = ((0, 2), (2, 1), (3, 1))
+TAIL_RATE = 4
+W0 = 3
+XF_ON_V = (0, 1)
+
+
+def tile_fr_pb_kernel(tc, x1, x2, FE_x1, FE_x2, g1, g2, p1_w, p1_b, p2_w, p2_b, out_0, out_1):
+    nc = tc.nc
+    xs = [a.rearrange("n (j p) h w -> n p j (h w)", p=P) for a in (x1, x2)]
+    fs = [a.rearrange("n (j p) h w -> n p j (h w)", p=P) for a in (FE_x1, FE_x2)]
+    ws = [a.rearrange("(m p) k -> p m k", p=P) for a in (p1_w, p2_w)]
+    os_ = [a.rearrange("n (m p) h w -> n m p (h w)", p=P) for a in (out_0, out_1)]
+    with ExitStack() as ctx:
+        const = ctx.enter_context(tc.tile_pool(name="const", bufs=1))
+        inp = ctx.enter_context(tc.tile_pool(name="inp", bufs=3))
+        cl = ctx.enter_context(tc.tile_pool(name="cl", bufs=2))
+        wk = ctx.enter_context(tc.tile_pool(name="wk", bufs=3))
+        sm = ctx.enter_context(tc.tile_pool(name="sm", bufs=4))
+        ps = ctx.enter_context(tc.psum_pool(name="ps", bufs=1))
+        ctx.enter_context(tc.manual_schedule())
+
+        st = {}
+
+        def load(g):
+            n, gh = divmod(g, 2)
+            cols = slice(GW * gh, GW * gh + GW)
+            for i in range(2):
+                t = inp.tile([P, J, GW], BF16, name="x%d" % i, tag="x%d" % i, bufs=4)
+                nc.sync.dma_start(out=t[:], in_=xs[i][n][:, :, cols])
+                st["x", g, i] = t
+            for i in range(2):
+                t = inp.tile([P, J, GW], BF16, name="f%d" % i, tag="f%d" % i, bufs=3)
+                nc.sync.dma_start(out=t[:], in_=fs[i][n][:, :, cols])
+                st["f", g, i] = t
+
+        def prod_y(g, on_v):
+            n = g // 2
+            for i in range(2):
+                y = cl.tile([P, J, GW], F32, name="y%d" % i, tag="y%d" % i)
+                st["y", g, i] = y
+                for j in range(J):
+                    sgc = sg[:, j, 4 * i + n : 4 * i + n + 1]
+                    if on_v:
+                        nc.vector.tensor_scalar(out=y[:, j, :], in0=st["x", g, i][:, j, :], scalar1=sgc, scalar2=None, op0=ALU.mult)
+                    else:
+                        nc.gpsimd.tensor_scalar(out=y[:, j, :], in0=st["x", g, i][:, j, :], scalar1=sgc, scalar2=0.0, op0=ALU.mult, op1=ALU.add)
+
+        def prod_xf(g):
+            xf = cl.tile([P, 2, GW], F32, name="xf", tag="xf")
+            st["xf", g] = xf
+            for i in range(2):
+                if g in XF_ON_V:
+                    nc.vector.tensor_copy(out=xf[:, i, :], in_=st["x", g, 1 - i][:, PLAIN_J, :])
+                else:
+                    nc.gpsimd.tensor_scalar(out=xf[:, i, :], in0=st["x", g, 1 - i][:, PLAIN_J, :], scalar1=1.0, scalar2=0.0, op0=ALU.mult, op1=ALU.add)
+
+        def prod_u(g, on_v, which=(0, 1)):
+            for i in which:
+                u = cl.tile([P, J, GW], F32, name="u%d" % i, tag="u%d" % i)
+                st["u", g, i] = u
+                eng = nc.vector if on_v else nc.gpsimd
+                eng.tensor_tensor(out=u[:], in0=st["x", g, 1 - i][:], in1=st["f", g, i][:], op=ALU.add)
+
+        def where(h):
+            t, i = divmod(h, 2)
+            g, b = divmod(t, 4)
+            return t, i, g, slice(P * b, P * b + P)
+
+        def pe_r(h):
+            t, i, g, cols = where(h)
+            r = ps.tile([P, GW], F32, name="r", tag="r", bufs=3)
+            st["r", h] = r
+            for j in range(J):
+                o = r[:, P * j : P * j + P]
+                nc.tensor.matmul(o, lhsT=st["y", g, i][:, j, cols], rhs=ident_f[:], is_transpose=True, start=True, stop=False)
+                if j < PLAIN_J:
+                    nc.tensor.matmul(o, lhsT=st["x", g, 1 - i][:, j, cols], rhs=ident_b[:], start=False, stop=True)
+                else:
+                    nc.tensor.matmul(o, lhsT=st["xf", g][:, i, cols], rhs=ident_f[:], is_transpose=True, start=False, stop=True)
+
+        def s_a(h):
+            a = wk.tile([P, GW], F32, name="a", tag="a")
+            st["a", h] = a
+            nc.scalar.activation(out=a[:], in_=st["r", h][:], func=ACT.Exp)
+
+        def v_max(h):
+            nm = sm.tile([P, 1], F32, name="nm", tag="nm")
+            st["nm", h] = nm
+            nc.vector.tensor_reduce(out=nm[:], in_=st["a", h][:], axis=AX.X, op=ALU.max, negate=True)
+
+        def s_e(h):
+            t, i, g, cols = where(h)
+            if i == 0:
+                st["se", t] = sm.tile([P, 2], F32, name="se", tag="se")
+            e = wk.tile([P, GW], F32, name="e", tag="e")
+            st["e", h] = e
+            nc.scalar.activation(out=e[:], in_=st["a", h][:], func=ACT.Exp, bias=st["nm", h][:], scale=1.0, accum_out=st["se", t][:, i : i + 1])
+
+        def v_ser(h):
+            t, i, g, cols = where(h)
+            if i == 0:
+                st["ser", t] = sm.tile([P, 2], F32, name="ser", tag="ser")
+            e = st["e", h]
+            nc.vector.scalar_tensor_tensor(out=e[:], in0=e[:], scalar=1.0, in1=st["r", h][:], op0=ALU.mult, op1=ALU.mult, accum_out=st["ser", t][:, i : i + 1])
+            if i == 1:
+                rse = sm.tile([P, 2], F32, name="rse", tag="rse")
+                s2 = sm.tile([P, 2], F32, name="s2", tag="s2")
+                st["s", t] = s2
+                nc.vector.reciprocal(out=rse[:], in_=st["se", t][:])
+                nc.vector.tensor_tensor(out=s2[:], in0=st["ser", t][:], in1=rse[:], op=ALU.mult)
+
+        def pe_x(t):
+            g, b = divmod(t, 4)
+            cols = slice(P * b, P * b + P)
+            x = ps.tile([P, 2, GW], BF16, name="xT", tag="xT", bufs=1)
+            st["xT", t] = x
+            for i in range(2):
+                for j in range(J):
+                    nc.tensor.transpose(out=x[:, i, P * j : P * j + P], in_=st["x", g, i][:, j, cols], identity=ident_b[:])
+
+        def s_t(h):
+            t, i, g, cols = where(h)
+            tt = wk.tile([P, GW], F32, name="tT", tag="tT")
+            st["tT", h] = tt
+            nc.scalar.activation(out=tt[:], in_=st["xT", t][:, i, :], func=ACT.Copy, scale=st["s", t][:, i : i + 1])
+
+        def pe_z(h):
+            z = ps.tile([P, J, P], F32, name="z", tag="z", bufs=2)
+            st["z", h] = z
+            for j in range(J):
+                nc.tensor.transpose(out=z[:, j, :], in_=st["tT", h][:, P * j : P * j + P], identity=ident_f[:])
+
+        def v_z(h):
+            t, i, g, cols = where(h)
+            if h % 8 == 0:
+                st["grp", g] = cl.tile([P, 2, GW, J], BF16, name="grp", tag="grp", align_bytes=64)
+            nc.vector.tensor_tensor(
+                out=st["grp", g][:, i, cols, :],
+                in0=st["z", h][:].rearrange("p j c -> p c j"),
+                in1=st["u", g, i][:, :, cols].rearrange("p j c -> p c j"),
+                op=ALU.add,
+            )
+
+        def v_q(ch):
+            g, u0, nu = ch
+            if u0 == 0:
+                st["codes", g] = cl.tile([P, 2 * GW], U32, name="codes", tag="codes", align_bytes=64)
+                st["scl", g] = cl.tile([P, 2 * GW], U8, name="scl", tag="scl", align_bytes=64)
+            codes, scl, grp = st["codes", g], st["scl", g], st["grp", g]
+            if nu == 4:
+                nc.vector.quantize_mx(out=codes[:].bitcast(FP8X4), scales=scl[:], in_=grp[:].rearrange("p i c j -> p (i c j)"))
+            else:
+                for s in range(2):
+                    c = slice(GW * s + P * u0, GW * s + P * (u0 + nu))
+                    nc.vector.quantize_mx(
+                        out=codes[:, c].bitcast(FP8X4), scales=scl[:, c],
+                        in_=grp[:, s, P * u0 : P * (u0 + nu), :].rearrange("p c j -> p (c j)"),
+                    )
+
+        def pe_m(ch, m8):
+            g, u0, nu = ch
+            m = ps.tile([P, GW], F32, name="m", tag="m", bufs=2)
+            st["m", ch, m8] = m
+            for s in range(2):
+                wc = slice((2 * m8 + s) * P, (2 * m8 + s) * P + P)
+                rc = slice(GW * s + P * u0, GW * s + P * (u0 + nu))
+                nc.tensor.matmul_mx(
+                    out=m[:, 0 : P * nu], lhsT=w_codes[:, wc].bitcast(FP8X4), lhsT_scale=w_scl[:, wc],
+                    rhs=st["codes", g][:, rc].bitcast(FP8X4), rhs_scale=st["scl", g][:, rc],
+                    start=(s == 0), stop=(s == 1),
+                )
+
+        def ev_m(ch, m8, on_v):
+            g, u0, nu = ch
+            n, gh = divmod(g, 2)
+            w, mm = divmod(m8, 4)
+            wd = P * nu
+            ob = wk.tile([P, GW], F32, name="ob", tag="ob", bufs=6)
+            b = bias[:, mm, w : w + 1]
+            if on_v:
+                nc.vector.tensor_scalar(out=ob[:, 0:wd], in0=st["m", ch, m8][:, 0:wd], scalar1=b, scalar2=None, op0=ALU.add)
+            else:
+                nc.scalar.activation(out=ob[:, 0:wd], in_=st["m", ch, m8][:, 0:wd], func=ACT.Identity, bias=b, scale=1.0)
+            c0 = GW * gh + P * u0
+            nc.sync.dma_start(out=os_[w][n, mm][:, c0 : c0 + wd], in_=ob[:, 0:wd])
+
+        gts = []
+        for nm_, src in (("ga", g1), ("gc", g2)):
+            t = const.tile([P, GW], BF16, name=nm_)
+            nc.vector.memset(t[:], 0.0)
+            nc.sync.dma_start(out=t[0:4, :], in_=src)
+            gts.append(t)
+        load(0)
+        bts = []
+        for nm_, src in (("ba", p1_b), ("bc", p2_b)):
+            t = const.tile([P, GW], BF16, name=nm_)
+            nc.vector.memset(t[:], 0.0)
+            nc.sync.dma_start(out=t[0:1, :], in_=src.rearrange("(o c) -> o c", o=1))
+            bts.append(t)
+        ident_b = const.tile([P, P], BF16, name="ident_b")
+        make_identity(nc, ident_b[:])
+        ident_f = const.tile([P, P], F32, name="ident_f")
+        make_identity(nc, ident_f[:])
+        load(1)
+        w_raw = []
+        for w in range(2):
+            t = const.tile([P, J, 1024], BF16, name="w_raw%d" % w)
+            nc.sync.dma_start(out=t[:], in_=ws[w])
+            w_raw.append(t)
+        load(2)
+
+        gT = ps.tile([P, 2, J, P], BF16, name="gT", tag="xT", bufs=1)
+        for i in range(2):
+            for j in range(J):
+                nc.tensor.transpose(out=gT[:, i, j, :], in_=gts[i][:, P * j : P * j + P], identity=ident_b[:])
+        sg = const.tile([P, J, 8], F32, name="sg")
+        for i in range(2):
+            nc.scalar.activation(out=sg[:, :, 4 * i : 4 * i + 4], in_=gT[:, i, :, 0:4], func=ACT.Exp, scale=-1.0)
+        nc.vector.tensor_scalar(out=sg[:], in0=sg[:], scalar1=1.0, scalar2=None, op0=ALU.add)
+        nc.vector.reciprocal(out=sg[:], in_=sg[:])
+        bias = const.tile([P, J, 2], F32, name="bias")
+
+        prod_y(0, True)
+        prod_xf(0)
+        prod_y(1, False)
+
+        w_codes = const.tile([P, 16 * P], U32, name="w_codes", align_bytes=64)
+        w_scl = const.tile([P, 16 * P], U8, name="w_scl", align_bytes=64)
+
+        def w_t(w, mm):
+            wT = ps.tile([P, 8, P], BF16, name="wT", tag="m", bufs=2)
+            st["wT", w, mm] = wT
+            for kk in range(8):
+                nc.tensor.transpose(out=wT[:, kk, :], in_=w_raw[w][:, mm, P * kk : P * kk + P], identity=ident_b[:])
+
+        def w_ev(w, mm):
+            if mm == 0:
+                st["wg", w] = const.tile([P, J, 2, P, 4], BF16, name="wg", tag="wg", align_bytes=64)
+            src = st["wT", w, mm][:].rearrange("p (s t) o -> p s o t", t=4)
+            if mm % 2 == 0:
+                nc.scalar.copy(out=st["wg", w][:, mm], in_=src)
+            else:
+                nc.vector.tensor_copy(out=st["wg", w][:, mm], in_=src)
+            if mm == 3:
+                c = slice(1024 * w, 1024 * w + 1024)
+                nc.vector.quantize_mx(out=w_codes[:, c].bitcast(FP8X4), scales=w_scl[:, c], in_=st["wg", w][:].rearrange("p m s o t -> p (m s o t)"))
+
+        chunks = [(g, 0, 4) for g in range(NG - 1)] + [(NG - 1, u0, nu) for (u0, nu) in LAST]
+        q_step = {}
+        for ch in chunks:
+            q_step[8 * ch[0] + 2 * (ch[1] + ch[2]) - 1 + L_Z + 1] = ch
+        jobs = []
+        done = 0
+        evd = 0
+
+        def on(h):
+            return 0 <= h < NH
+
+        pe_r(0)
+        k = 0
+        while k < NH + L_Z + 2 or evd < len(jobs):
+            if on(k - L_SER):
+                v_ser(k - L_SER)
+            if on(k):
+                s_a(k)
+            if on(k - L_E):
+                s_e(k - L_E)
+            if on(k - L_Z):
+                v_z(k - L_Z)
+            if on(k):
+                v_max(k)
+            if on(k - L_T):
+                s_t(k - L_T)
+            if W0 < k <= W0 + 8:
+                w_ev((k - W0 - 1) // 4, (k - W0 - 1) % 4)
+            for jj in range(1 if k < NH else TAIL_RATE):
+                if done < len(jobs):
+                    pe_m(jobs[done][0], jobs[done][1])
+                    done += 1
+                if evd < done - 1 or (evd < done and done == len(jobs)):
+                    ev_m(jobs[evd][0], jobs[evd][1], (jobs[evd][1] in V_EV) if k < NH else (evd % 2 == 1))
+                    evd += 1
+            if k in q_step:
+                v_q(q_step[k])
+                jobs.extend([(q_step[k], m8) for m8 in range(8)])
+            if on(k + 1):
+                pe_r(k + 1)
+            if on(k - L_T):
+                pe_z(k - L_T)
+            if (k - L_T) % 2 == 1 and on(k - L_T + 1):
+                pe_x((k - L_T + 1) // 2)
+            if k == L_T - 2:
+                pe_x(0)
+            if W0 <= k < W0 + 8:
+                w_t((k - W0) // 4, (k - W0) % 4)
+            if k == 2:
+                bT = ps.tile([P, 2, J, P], BF16, name="bT", tag="m", bufs=2)
+                for w in range(2):
+                    for j in range(J):
+                        nc.tensor.transpose(out=bT[:, w, j, :], in_=bts[w][:, P * j : P * j + P], identity=ident_b[:])
+                for w in range(2):
+                    nc.vector.tensor_copy(out=bias[:, :, w : w + 1], in_=bT[:, w, :, 0:1])
+            if k in (1, 2):
+                prod_u(0, True, (k - 1,))
+            if k == 2:
+                prod_u(1, False)
+            gk, rk = divmod(k, 8)
+            if rk == 0 and 2 <= gk + 1 < NG:
+                prod_y(gk + 1, False)
+            if rk == 3 and gk + 1 < NG:
+                prod_xf(gk + 1)
+            if rk == L_Z + 1 and 2 <= gk + 1 < NG:
+                prod_u(gk + 1, False)
+            if rk == L_T + 2 and gk + 3 < NG:
+                load(gk + 3)
+            k += 1

@@ -19,15 +19,28 @@ J = 4
 GW = 512
 NG = 8
 NH = 64
-L_E = 1
-L_SER = 2
-L_T = 4
-L_Z = 5
-L_Q = 6
+ORDER = (
+    ("s_a", 0), ("s_e", 1), ("v_z", 6), ("v_max", 0), ("v_ser", 1), ("s_t", 4), ("w_ev", 0),
+    ("pe_z", 5), ("pe_r", -1), ("pe_m", 0), ("ev_m", 0), ("v_q", 0), ("pe_x", 3), ("w_t", 0), ("misc", 0),
+)
+DUMMY = 0
+RAMP_DUMMY = 0
+R_BUFS = 3
+X_BUFS = 1
+Z_BUFS = 2
+M_BUFS = 2
+Y_STEP = 0
+U_STEP = 7
+XF_STEP = 3
+LD_STEP = 6
 PLAIN_J = 3
 V_EV = (3, 7)
-LAST = ((0, 2), (2, 1), (3, 1))
+LAST = ((0, 2), (2, 2))
 TAIL_RATE = 4
+TAIL_TAGS = ("m", "r", "m", "r", "r")
+TAIL_LAG = 4
+MID_RATE = 2
+TAIL_AT = 7
 W0 = 3
 XF_ON_V = (0, 1)
 
@@ -96,9 +109,9 @@ def tile_fr_pb_kernel(tc, x1, x2, FE_x1, FE_x2, g1, g2, p1_w, p1_b, p2_w, p2_b, 
 
         def pe_r(h):
             t, i, g, cols = where(h)
-            r = ps.tile([P, GW], F32, name="r", tag="r", bufs=3)
+            r = ps.tile([P, GW], F32, name="r", tag="r", bufs=R_BUFS)
             st["r", h] = r
-            for j in range(J):
+            for j in (3, 0, 1, 2):
                 o = r[:, P * j : P * j + P]
                 nc.tensor.matmul(o, lhsT=st["y", g, i][:, j, cols], rhs=ident_f[:], is_transpose=True, start=True, stop=False)
                 if j < PLAIN_J:
@@ -140,7 +153,7 @@ def tile_fr_pb_kernel(tc, x1, x2, FE_x1, FE_x2, g1, g2, p1_w, p1_b, p2_w, p2_b, 
         def pe_x(t):
             g, b = divmod(t, 4)
             cols = slice(P * b, P * b + P)
-            x = ps.tile([P, 2, GW], BF16, name="xT", tag="xT", bufs=1)
+            x = ps.tile([P, 2, GW], BF16, name="xT", tag="xT", bufs=X_BUFS)
             st["xT", t] = x
             for i in range(2):
                 for j in range(J):
@@ -153,7 +166,7 @@ def tile_fr_pb_kernel(tc, x1, x2, FE_x1, FE_x2, g1, g2, p1_w, p1_b, p2_w, p2_b, 
             nc.scalar.activation(out=tt[:], in_=st["xT", t][:, i, :], func=ACT.Copy, scale=st["s", t][:, i : i + 1])
 
         def pe_z(h):
-            z = ps.tile([P, J, P], F32, name="z", tag="z", bufs=2)
+            z = ps.tile([P, J, P], F32, name="z", tag="z", bufs=Z_BUFS)
             st["z", h] = z
             for j in range(J):
                 nc.tensor.transpose(out=z[:, j, :], in_=st["tT", h][:, P * j : P * j + P], identity=ident_f[:])
@@ -185,10 +198,18 @@ def tile_fr_pb_kernel(tc, x1, x2, FE_x1, FE_x2, g1, g2, p1_w, p1_b, p2_w, p2_b, 
                         in_=grp[:, s, P * u0 : P * (u0 + nu), :].rearrange("p c j -> p (c j)"),
                     )
 
-        def pe_m(ch, m8):
+        def pe_m(ch, m8, tag):
             g, u0, nu = ch
-            m = ps.tile([P, GW], F32, name="m", tag="m", bufs=2)
+            m = ps.tile([P, GW], F32, name="m", tag=tag, bufs=(M_BUFS if tag == "m" else R_BUFS))
             st["m", ch, m8] = m
+            for d in range(DUMMY):
+                wc = slice(2 * m8 * P, 2 * m8 * P + P)
+                rc = slice(P * u0, P * (u0 + nu))
+                nc.tensor.matmul_mx(
+                    out=m[:, 0 : P * nu], lhsT=w_codes[:, wc].bitcast(FP8X4), lhsT_scale=w_scl[:, wc],
+                    rhs=st["codes", g][:, rc].bitcast(FP8X4), rhs_scale=st["scl", g][:, rc],
+                    start=True, stop=True,
+                )
             for s in range(2):
                 wc = slice((2 * m8 + s) * P, (2 * m8 + s) * P + P)
                 rc = slice(GW * s + P * u0, GW * s + P * (u0 + nu))
@@ -237,7 +258,7 @@ def tile_fr_pb_kernel(tc, x1, x2, FE_x1, FE_x2, g1, g2, p1_w, p1_b, p2_w, p2_b, 
             w_raw.append(t)
         load(2)
 
-        gT = ps.tile([P, 2, J, P], BF16, name="gT", tag="xT", bufs=1)
+        gT = ps.tile([P, 2, J, P], BF16, name="gT", tag="xT", bufs=X_BUFS)
         for i in range(2):
             for j in range(J):
                 nc.tensor.transpose(out=gT[:, i, j, :], in_=gts[i][:, P * j : P * j + P], identity=ident_b[:])
@@ -252,11 +273,16 @@ def tile_fr_pb_kernel(tc, x1, x2, FE_x1, FE_x2, g1, g2, p1_w, p1_b, p2_w, p2_b, 
         prod_xf(0)
         prod_y(1, False)
 
+        if RAMP_DUMMY:
+            zc = const.tile([P, GW], U32, name="zc", align_bytes=64)
+            zs = const.tile([P, GW], U8, name="zs", align_bytes=64)
+            nc.vector.memset(zc[:].bitcast(mybir.dt.int32), 0)
+            nc.vector.memset(zs[:].bitcast(mybir.dt.int32), 0)
         w_codes = const.tile([P, 16 * P], U32, name="w_codes", align_bytes=64)
         w_scl = const.tile([P, 16 * P], U8, name="w_scl", align_bytes=64)
 
         def w_t(w, mm):
-            wT = ps.tile([P, 8, P], BF16, name="wT", tag="m", bufs=2)
+            wT = ps.tile([P, 8, P], BF16, name="wT", tag="m", bufs=M_BUFS)
             st["wT", w, mm] = wT
             for kk in range(8):
                 nc.tensor.transpose(out=wT[:, kk, :], in_=w_raw[w][:, mm, P * kk : P * kk + P], identity=ident_b[:])
@@ -274,55 +300,43 @@ def tile_fr_pb_kernel(tc, x1, x2, FE_x1, FE_x2, g1, g2, p1_w, p1_b, p2_w, p2_b, 
                 nc.vector.quantize_mx(out=w_codes[:, c].bitcast(FP8X4), scales=w_scl[:, c], in_=st["wg", w][:].rearrange("p m s o t -> p (m s o t)"))
 
         chunks = [(g, 0, 4) for g in range(NG - 1)] + [(NG - 1, u0, nu) for (u0, nu) in LAST]
-        q_step = {}
-        for ch in chunks:
-            q_step[8 * ch[0] + 2 * (ch[1] + ch[2]) - 1 + L_Z + 1] = ch
+        cnt = {"z": 0, "q": 0, "done": 0, "evd": 0}
         jobs = []
-        done = 0
-        evd = 0
 
         def on(h):
             return 0 <= h < NH
 
-        pe_r(0)
-        k = 0
-        while k < NH + L_Z + 2 or evd < len(jobs):
-            if on(k - L_SER):
-                v_ser(k - L_SER)
-            if on(k):
-                s_a(k)
-            if on(k - L_E):
-                s_e(k - L_E)
-            if on(k - L_Z):
-                v_z(k - L_Z)
-            if on(k):
-                v_max(k)
-            if on(k - L_T):
-                s_t(k - L_T)
-            if W0 < k <= W0 + 8:
-                w_ev((k - W0 - 1) // 4, (k - W0 - 1) % 4)
-            for jj in range(1 if k < NH else TAIL_RATE):
-                if done < len(jobs):
-                    pe_m(jobs[done][0], jobs[done][1])
-                    done += 1
-                if evd < done - 1 or (evd < done and done == len(jobs)):
-                    ev_m(jobs[evd][0], jobs[evd][1], (jobs[evd][1] in V_EV) if k < NH else (evd % 2 == 1))
-                    evd += 1
-            if k in q_step:
-                v_q(q_step[k])
-                jobs.extend([(q_step[k], m8) for m8 in range(8)])
-            if on(k + 1):
-                pe_r(k + 1)
-            if on(k - L_T):
-                pe_z(k - L_T)
-            if (k - L_T) % 2 == 1 and on(k - L_T + 1):
-                pe_x((k - L_T + 1) // 2)
-            if k == L_T - 2:
-                pe_x(0)
-            if W0 <= k < W0 + 8:
-                w_t((k - W0) // 4, (k - W0) % 4)
+        def do_q():
+            if cnt["q"] < len(chunks):
+                ch = chunks[cnt["q"]]
+                if cnt["z"] >= 8 * ch[0] + 2 * (ch[1] + ch[2]):
+                    v_q(ch)
+                    jobs.extend([(ch, m8) for m8 in range(8)])
+                    cnt["q"] += 1
+
+        def do_m():
+            if cnt["done"] >= cnt["avail"] and cnt["q"] == 0 and RAMP_DUMMY:
+                m = ps.tile([P, GW], F32, name="m", tag="m", bufs=M_BUFS)
+                for d in range(RAMP_DUMMY):
+                    nc.tensor.matmul_mx(
+                        out=m[:], lhsT=zc[:, 0:P].bitcast(FP8X4), lhsT_scale=zs[:, 0:P],
+                        rhs=zc[:].bitcast(FP8X4), rhs_scale=zs[:], start=True, stop=True,
+                    )
+            if cnt["done"] < cnt["avail"]:
+                tail = cnt["k"] >= NH
+                pe_m(jobs[cnt["done"]][0], jobs[cnt["done"]][1], TAIL_TAGS[cnt["done"] % len(TAIL_TAGS)] if tail else "m")
+                cnt["done"] += 1
+
+        def do_ev(k):
+            e = cnt["evd"]
+            lag = 1 if k < NH + 1 else TAIL_LAG
+            if e < cnt["done"] - lag or (e < cnt["done"] and cnt["done"] == len(jobs)):
+                ev_m(jobs[e][0], jobs[e][1], (jobs[e][1] in V_EV) if k < NH else (e % 2 == 1))
+                cnt["evd"] += 1
+
+        def misc(k):
             if k == 2:
-                bT = ps.tile([P, 2, J, P], BF16, name="bT", tag="m", bufs=2)
+                bT = ps.tile([P, 2, J, P], BF16, name="bT", tag="m", bufs=M_BUFS)
                 for w in range(2):
                     for j in range(J):
                         nc.tensor.transpose(out=bT[:, w, j, :], in_=bts[w][:, P * j : P * j + P], identity=ident_b[:])
@@ -333,12 +347,52 @@ def tile_fr_pb_kernel(tc, x1, x2, FE_x1, FE_x2, g1, g2, p1_w, p1_b, p2_w, p2_b, 
             if k == 2:
                 prod_u(1, False)
             gk, rk = divmod(k, 8)
-            if rk == 0 and 2 <= gk + 1 < NG:
+            if rk == Y_STEP and 2 <= gk + 1 < NG:
                 prod_y(gk + 1, False)
-            if rk == 3 and gk + 1 < NG:
+            if rk == XF_STEP and gk + 1 < NG:
                 prod_xf(gk + 1)
-            if rk == L_Z + 1 and 2 <= gk + 1 < NG:
+            if rk == U_STEP and 2 <= gk + 1 < NG:
                 prod_u(gk + 1, False)
-            if rk == L_T + 2 and gk + 3 < NG:
+            if rk == LD_STEP and gk + 3 < NG:
                 load(gk + 3)
+
+        simple = {"v_ser": v_ser, "s_a": s_a, "s_e": s_e, "v_max": v_max, "s_t": s_t, "pe_r": pe_r, "pe_z": pe_z}
+        lag_r = [lag for (nm_, lag) in ORDER if nm_ == "pe_r"][0]
+        lag_x = [lag for (nm_, lag) in ORDER if nm_ == "pe_x"][0]
+        for h in range(-lag_r):
+            pe_r(h)
+        k = 0
+        while cnt["evd"] < 8 * len(chunks):
+            cnt["avail"] = len(jobs)
+            cnt["k"] = k
+            for rep in range(1 if k < NH else (MID_RATE if k < NH + TAIL_AT else TAIL_RATE)):
+                for (nm_, lag) in ORDER:
+                    h = k - lag
+                    if nm_ == "pe_m":
+                        do_m()
+                    elif nm_ == "ev_m":
+                        do_ev(k)
+                    elif rep > 0:
+                        continue
+                    elif nm_ in simple:
+                        if on(h):
+                            simple[nm_](h)
+                    elif nm_ == "v_z":
+                        if on(h):
+                            v_z(h)
+                            cnt["z"] += 1
+                    elif nm_ == "v_q":
+                        do_q()
+                    elif nm_ == "pe_x":
+                        if h % 2 == 0 and on(h):
+                            pe_x(h // 2)
+                    elif nm_ == "w_t":
+                        if W0 <= k < W0 + 8:
+                            w_t((k - W0) // 4, (k - W0) % 4)
+                    elif nm_ == "w_ev":
+                        if W0 < k <= W0 + 8:
+                            w_ev((k - W0 - 1) // 4, (k - W0 - 1) % 4)
+                    elif nm_ == "misc":
+                        misc(k)
+                cnt["avail"] = len(jobs)
             k += 1

@@ -23,7 +23,9 @@ ORDER = (
     ("s_a", 0), ("s_e", 1), ("v_z", 6), ("v_max", 0), ("v_ser", 1), ("s_t", 4), ("w_ev", 0),
     ("pe_z", 5), ("pe_r", -1), ("pe_m", 0), ("ev_m", 0), ("v_q", 0), ("pe_x", 3), ("w_t", 0), ("misc", 0),
 )
-DUMMY = 0
+DUMMY = 1
+MX_EVERY = 1
+SANDWICH = 0
 RAMP_DUMMY = 0
 R_BUFS = 3
 X_BUFS = 1
@@ -113,11 +115,17 @@ def tile_fr_pb_kernel(tc, x1, x2, FE_x1, FE_x2, g1, g2, p1_w, p1_b, p2_w, p2_b, 
             st["r", h] = r
             for j in (3, 0, 1, 2):
                 o = r[:, P * j : P * j + P]
-                nc.tensor.matmul(o, lhsT=st["y", g, i][:, j, cols], rhs=ident_f[:], is_transpose=True, start=True, stop=False)
-                if j < PLAIN_J:
-                    nc.tensor.matmul(o, lhsT=st["x", g, 1 - i][:, j, cols], rhs=ident_b[:], start=False, stop=True)
-                else:
+                yT = st["y", g, i][:, j, cols]
+                if j == PLAIN_J:
+                    nc.tensor.matmul(o, lhsT=yT, rhs=ident_f[:], is_transpose=True, start=True, stop=False)
                     nc.tensor.matmul(o, lhsT=st["xf", g][:, i, cols], rhs=ident_f[:], is_transpose=True, start=False, stop=True)
+                elif j == 2 and SANDWICH:
+                    do_m()
+                    nc.tensor.matmul(o, lhsT=st["x", g, 1 - i][:, j, cols], rhs=ident_b[:], start=True, stop=False)
+                    nc.tensor.matmul(o, lhsT=yT, rhs=ident_f[:], is_transpose=True, start=False, stop=True)
+                else:
+                    nc.tensor.matmul(o, lhsT=yT, rhs=ident_f[:], is_transpose=True, start=True, stop=False)
+                    nc.tensor.matmul(o, lhsT=st["x", g, 1 - i][:, j, cols], rhs=ident_b[:], start=False, stop=True)
 
         def s_a(h):
             a = wk.tile([P, GW], F32, name="a", tag="a")
@@ -300,8 +308,9 @@ def tile_fr_pb_kernel(tc, x1, x2, FE_x1, FE_x2, g1, g2, p1_w, p1_b, p2_w, p2_b, 
                 nc.vector.quantize_mx(out=w_codes[:, c].bitcast(FP8X4), scales=w_scl[:, c], in_=st["wg", w][:].rearrange("p m s o t -> p (m s o t)"))
 
         chunks = [(g, 0, 4) for g in range(NG - 1)] + [(NG - 1, u0, nu) for (u0, nu) in LAST]
-        cnt = {"z": 0, "q": 0, "done": 0, "evd": 0}
+        cnt = {"z": 0, "q": 0, "done": 0, "evd": 0, "k": 0, "avail": 0}
         jobs = []
+        istep = []
 
         def on(h):
             return 0 <= h < NH
@@ -315,6 +324,12 @@ def tile_fr_pb_kernel(tc, x1, x2, FE_x1, FE_x2, g1, g2, p1_w, p1_b, p2_w, p2_b, 
                     cnt["q"] += 1
 
         def do_m():
+            if cnt["k"] < NH and cnt["k"] % MX_EVERY != 0:
+                return
+            for rep2 in range(MX_EVERY if cnt["k"] < NH else 1):
+                do_m1()
+
+        def do_m1():
             if cnt["done"] >= cnt["avail"] and cnt["q"] == 0 and RAMP_DUMMY:
                 m = ps.tile([P, GW], F32, name="m", tag="m", bufs=M_BUFS)
                 for d in range(RAMP_DUMMY):
@@ -325,12 +340,13 @@ def tile_fr_pb_kernel(tc, x1, x2, FE_x1, FE_x2, g1, g2, p1_w, p1_b, p2_w, p2_b, 
             if cnt["done"] < cnt["avail"]:
                 tail = cnt["k"] >= NH
                 pe_m(jobs[cnt["done"]][0], jobs[cnt["done"]][1], TAIL_TAGS[cnt["done"] % len(TAIL_TAGS)] if tail else "m")
+                istep.append(cnt["k"])
                 cnt["done"] += 1
 
         def do_ev(k):
             e = cnt["evd"]
             lag = 1 if k < NH + 1 else TAIL_LAG
-            if e < cnt["done"] - lag or (e < cnt["done"] and cnt["done"] == len(jobs)):
+            if e < cnt["done"] - lag or (e < cnt["done"] and (cnt["done"] == len(jobs) or istep[e] < k)):
                 ev_m(jobs[e][0], jobs[e][1], (jobs[e][1] in V_EV) if k < NH else (e % 2 == 1))
                 cnt["evd"] += 1
 
@@ -369,7 +385,8 @@ def tile_fr_pb_kernel(tc, x1, x2, FE_x1, FE_x2, g1, g2, p1_w, p1_b, p2_w, p2_b, 
                 for (nm_, lag) in ORDER:
                     h = k - lag
                     if nm_ == "pe_m":
-                        do_m()
+                        if not (SANDWICH and on(k - lag_r)):
+                            do_m()
                     elif nm_ == "ev_m":
                         do_ev(k)
                     elif rep > 0:

@@ -23,8 +23,10 @@ ORDER = (
     ("s_a", 0), ("s_e", 1), ("v_z", 6), ("v_max", 0), ("v_ser", 1), ("s_t", 4), ("w_ev", 0),
     ("pe_z", 5), ("pe_r", -1), ("pe_m", 0), ("ev_m", 0), ("v_q", 0), ("pe_x", 3), ("w_t", 0), ("misc", 0),
 )
-DUMMY = 1
+DUMMY = 0
 MX_EVERY = 1
+Y_V = 1
+U_SPLIT = 1
 SANDWICH = 0
 RAMP_DUMMY = 0
 R_BUFS = 3
@@ -88,6 +90,20 @@ def tile_fr_pb_kernel(tc, x1, x2, FE_x1, FE_x2, g1, g2, p1_w, p1_b, p2_w, p2_b, 
                     else:
                         nc.gpsimd.tensor_scalar(out=y[:, j, :], in0=st["x", g, i][:, j, :], scalar1=sgc, scalar2=0.0, op0=ALU.mult, op1=ALU.add)
 
+        def y_piece(g, idx):
+            n = g // 2
+            i, j = divmod(idx, J)
+            if j == 0:
+                st["y", g, i] = cl.tile([P, J, GW], F32, name="y%d" % i, tag="y%d" % i)
+            nc.vector.tensor_scalar(
+                out=st["y", g, i][:, j, :], in0=st["x", g, i][:, j, :], scalar1=sg[:, j, 4 * i + n : 4 * i + n + 1], scalar2=None, op0=ALU.mult
+            )
+
+        def xf_piece(g, i):
+            if i == 0:
+                st["xf", g] = cl.tile([P, 2, GW], F32, name="xf", tag="xf")
+            nc.vector.tensor_copy(out=st["xf", g][:, i, :], in_=st["x", g, 1 - i][:, PLAIN_J, :])
+
         def prod_xf(g):
             xf = cl.tile([P, 2, GW], F32, name="xf", tag="xf")
             st["xf", g] = xf
@@ -102,7 +118,8 @@ def tile_fr_pb_kernel(tc, x1, x2, FE_x1, FE_x2, g1, g2, p1_w, p1_b, p2_w, p2_b, 
                 u = cl.tile([P, J, GW], F32, name="u%d" % i, tag="u%d" % i)
                 st["u", g, i] = u
                 eng = nc.vector if on_v else nc.gpsimd
-                eng.tensor_tensor(out=u[:], in0=st["x", g, 1 - i][:], in1=st["f", g, i][:], op=ALU.add)
+                for j0 in range(0, J, U_SPLIT):
+                    eng.tensor_tensor(out=u[:, j0 : j0 + U_SPLIT, :], in0=st["x", g, 1 - i][:, j0 : j0 + U_SPLIT, :], in1=st["f", g, i][:, j0 : j0 + U_SPLIT, :], op=ALU.add)
 
         def where(h):
             t, i = divmod(h, 2)
@@ -279,7 +296,8 @@ def tile_fr_pb_kernel(tc, x1, x2, FE_x1, FE_x2, g1, g2, p1_w, p1_b, p2_w, p2_b, 
 
         prod_y(0, True)
         prod_xf(0)
-        prod_y(1, False)
+        if not Y_V:
+            prod_y(1, False)
 
         if RAMP_DUMMY:
             zc = const.tile([P, GW], U32, name="zc", align_bytes=64)
@@ -363,10 +381,16 @@ def tile_fr_pb_kernel(tc, x1, x2, FE_x1, FE_x2, g1, g2, p1_w, p1_b, p2_w, p2_b, 
             if k == 2:
                 prod_u(1, False)
             gk, rk = divmod(k, 8)
-            if rk == Y_STEP and 2 <= gk + 1 < NG:
-                prod_y(gk + 1, False)
-            if rk == XF_STEP and gk + 1 < NG:
-                prod_xf(gk + 1)
+            if Y_V:
+                if gk + 1 < NG:
+                    y_piece(gk + 1, rk)
+                    if rk in (2, 5):
+                        xf_piece(gk + 1, rk // 4)
+            else:
+                if rk == Y_STEP and 2 <= gk + 1 < NG:
+                    prod_y(gk + 1, False)
+                if rk == XF_STEP and gk + 1 < NG:
+                    prod_xf(gk + 1)
             if rk == U_STEP and 2 <= gk + 1 < NG:
                 prod_u(gk + 1, False)
             if rk == LD_STEP and gk + 3 < NG:

@@ -15,262 +15,220 @@ AX = mybir.AxisListType
 FLOPS = 2 * 1024 * 1024 * 4096
 
 P = 128
-J = 4
-GW = 512
-NG = 8
-NH = 64
-ORDER = (
-    ("s_a", 0), ("s_e", 1), ("v_z", 6), ("v_max", 0), ("v_ser", 1), ("s_t", 4), ("w_ev", 0),
-    ("pe_z", 5), ("pe_r", -1), ("pe_m", 0), ("ev_m", 0), ("v_q", 0), ("pe_x", 3), ("w_t", 0), ("misc", 0),
-)
-DUMMY = 0
-MX_EVERY = 1
-Y_V = 1
-U_SPLIT = 1
-SANDWICH = 0
-RAMP_DUMMY = 0
-R_BUFS = 3
-X_BUFS = 1
-Z_BUFS = 2
-M_BUFS = 2
-Y_STEP = 0
-U_STEP = 7
-XF_STEP = 3
-LD_STEP = 6
-PLAIN_J = 3
-V_EV = (3, 7)
-LAST = ((0, 2), (2, 2))
-TAIL_RATE = 4
-TAIL_TAGS = ("m", "r", "m", "r", "r")
-TAIL_LAG = 4
-MID_RATE = 2
-TAIL_AT = 7
-W0 = 3
-XF_ON_V = (0, 1)
+PACK = 4
+GROUP = 512
+STEPS = 64
+GROUPS = 8
+TILES = 8
+PLAIN = 3
 
 
 def tile_fr_pb_kernel(tc, x1, x2, FE_x1, FE_x2, g1, g2, p1_w, p1_b, p2_w, p2_b, out_0, out_1):
     nc = tc.nc
-    xs = [a.rearrange("n (j p) h w -> n p j (h w)", p=P) for a in (x1, x2)]
-    fs = [a.rearrange("n (j p) h w -> n p j (h w)", p=P) for a in (FE_x1, FE_x2)]
-    ws = [a.rearrange("(m p) k -> p m k", p=P) for a in (p1_w, p2_w)]
-    os_ = [a.rearrange("n (m p) h w -> n m p (h w)", p=P) for a in (out_0, out_1)]
+    x_hbm = [a.rearrange("n (p j) h w -> n p j (h w)", j=PACK) for a in (x1, x2)]
+    fe_hbm = [a.rearrange("n (p j) h w -> n p j (h w)", j=PACK) for a in (FE_x1, FE_x2)]
+    w_hbm = [a.rearrange("(m p) k -> p m k", p=P) for a in (p1_w, p2_w)]
+    out_hbm = [a.rearrange("n (m p) h w -> n m p (h w)", p=P) for a in (out_0, out_1)]
+
     with ExitStack() as ctx:
         const = ctx.enter_context(tc.tile_pool(name="const", bufs=1))
-        inp = ctx.enter_context(tc.tile_pool(name="inp", bufs=3))
-        cl = ctx.enter_context(tc.tile_pool(name="cl", bufs=2))
-        wk = ctx.enter_context(tc.tile_pool(name="wk", bufs=3))
-        sm = ctx.enter_context(tc.tile_pool(name="sm", bufs=4))
-        ps = ctx.enter_context(tc.psum_pool(name="ps", bufs=1))
+        groups = ctx.enter_context(tc.tile_pool(name="groups", bufs=2))
+        steps = ctx.enter_context(tc.tile_pool(name="steps", bufs=3))
+        small = ctx.enter_context(tc.tile_pool(name="small", bufs=4))
+        psum = ctx.enter_context(tc.psum_pool(name="psum", bufs=1))
         ctx.enter_context(tc.manual_schedule())
 
-        st = {}
+        live = {}
+
+        def place(h):
+            block, i = divmod(h, 2)
+            g, b = divmod(block, 4)
+            return block, i, g, slice(P * b, P * b + P)
+
 
         def load(g):
-            n, gh = divmod(g, 2)
-            cols = slice(GW * gh, GW * gh + GW)
-            for i in range(2):
-                t = inp.tile([P, J, GW], BF16, name="x%d" % i, tag="x%d" % i, bufs=4)
-                nc.sync.dma_start(out=t[:], in_=xs[i][n][:, :, cols])
-                st["x", g, i] = t
-            for i in range(2):
-                t = inp.tile([P, J, GW], BF16, name="f%d" % i, tag="f%d" % i, bufs=3)
-                nc.sync.dma_start(out=t[:], in_=fs[i][n][:, :, cols])
-                st["f", g, i] = t
+            n, half = divmod(g, 2)
+            cols = slice(GROUP * half, GROUP * half + GROUP)
+            for kind, hbm, bufs in (("x", x_hbm, 4), ("fe", fe_hbm, 3)):
+                for i in range(2):
+                    t = groups.tile([P, PACK, GROUP], BF16, name="%s%d" % (kind, i), tag="%s%d" % (kind, i), bufs=bufs)
+                    nc.sync.dma_start(out=t[:], in_=hbm[i][n][:, :, cols])
+                    live[kind, g, i] = t
 
-        def prod_y(g, on_v):
+        def gate(g, i):
             n = g // 2
-            for i in range(2):
-                y = cl.tile([P, J, GW], F32, name="y%d" % i, tag="y%d" % i)
-                st["y", g, i] = y
-                for j in range(J):
-                    sgc = sg[:, j, 4 * i + n : 4 * i + n + 1]
-                    if on_v:
-                        nc.vector.tensor_scalar(out=y[:, j, :], in0=st["x", g, i][:, j, :], scalar1=sgc, scalar2=None, op0=ALU.mult)
-                    else:
-                        nc.gpsimd.tensor_scalar(out=y[:, j, :], in0=st["x", g, i][:, j, :], scalar1=sgc, scalar2=0.0, op0=ALU.mult, op1=ALU.add)
+            y = groups.tile([P, PACK, GROUP], F32, name="y%d" % i, tag="y%d" % i)
+            live["y", g, i] = y
+            for j in range(PACK):
+                nc.vector.tensor_scalar(
+                    out=y[:, j, :], in0=live["x", g, i][:, j, :], scalar1=sig[:, j, 4 * i + n : 4 * i + n + 1], scalar2=None, op0=ALU.mult
+                )
 
-        def y_piece(g, idx):
-            n = g // 2
-            i, j = divmod(idx, J)
-            if j == 0:
-                st["y", g, i] = cl.tile([P, J, GW], F32, name="y%d" % i, tag="y%d" % i)
-            nc.vector.tensor_scalar(
-                out=st["y", g, i][:, j, :], in0=st["x", g, i][:, j, :], scalar1=sg[:, j, 4 * i + n : 4 * i + n + 1], scalar2=None, op0=ALU.mult
+        def widen(g):
+            xf = groups.tile([P, 2, GROUP], F32, name="xf", tag="xf")
+            live["xf", g] = xf
+            for i in range(2):
+                nc.gpsimd.tensor_scalar(out=xf[:, i, :], in0=live["x", g, 1 - i][:, PLAIN, :], scalar1=1.0, scalar2=0.0, op0=ALU.mult, op1=ALU.add)
+
+        def rest(g):
+            for i in range(2):
+                u = groups.tile([P, PACK, GROUP], F32, name="u%d" % i, tag="u%d" % i)
+                live["u", g, i] = u
+                for j in range(PACK):
+                    nc.gpsimd.tensor_tensor(out=u[:, j, :], in0=live["x", g, 1 - i][:, j, :], in1=live["fe", g, i][:, j, :], op=ALU.add)
+
+
+        def r_to_positions(h):
+            block, i, g, cols = place(h)
+            r = psum.tile([P, PACK * P], F32, name="r", tag="r", bufs=3)
+            live["r", h] = r
+            for j in (PLAIN, 0, 1, 2):
+                o = r[:, P * j : P * j + P]
+                nc.tensor.matmul(o, lhsT=live["y", g, i][:, j, cols], rhs=ident_f[:], is_transpose=True, start=True, stop=False)
+                if j < PLAIN:
+                    nc.tensor.matmul(o, lhsT=live["x", g, 1 - i][:, j, cols], rhs=ident_b[:], start=False, stop=True)
+                else:
+                    nc.tensor.matmul(o, lhsT=live["xf", g][:, i, cols], rhs=ident_f[:], is_transpose=True, start=False, stop=True)
+
+        def exp_r(h):
+            a = steps.tile([P, PACK * P], F32, name="a", tag="a")
+            live["a", h] = a
+            nc.scalar.activation(out=a[:], in_=live["r", h][:], func=ACT.Exp)
+
+        def neg_max(h):
+            m = small.tile([P, 1], F32, name="negmax", tag="negmax")
+            live["negmax", h] = m
+            nc.vector.tensor_reduce(out=m[:], in_=live["a", h][:], axis=AX.X, op=ALU.max, negate=True)
+
+        def exp_shifted(h):
+            block, i, g, cols = place(h)
+            if i == 0:
+                live["sum_e", block] = small.tile([P, 2], F32, name="sum_e", tag="sum_e")
+            e = steps.tile([P, PACK * P], F32, name="e", tag="e")
+            live["e", h] = e
+            nc.scalar.activation(
+                out=e[:], in_=live["a", h][:], func=ACT.Exp, bias=live["negmax", h][:], scale=1.0, accum_out=live["sum_e", block][:, i : i + 1]
             )
 
-        def xf_piece(g, i):
+        def weigh(h):
+            block, i, g, cols = place(h)
             if i == 0:
-                st["xf", g] = cl.tile([P, 2, GW], F32, name="xf", tag="xf")
-            nc.vector.tensor_copy(out=st["xf", g][:, i, :], in_=st["x", g, 1 - i][:, PLAIN_J, :])
-
-        def prod_xf(g):
-            xf = cl.tile([P, 2, GW], F32, name="xf", tag="xf")
-            st["xf", g] = xf
-            for i in range(2):
-                if g in XF_ON_V:
-                    nc.vector.tensor_copy(out=xf[:, i, :], in_=st["x", g, 1 - i][:, PLAIN_J, :])
-                else:
-                    nc.gpsimd.tensor_scalar(out=xf[:, i, :], in0=st["x", g, 1 - i][:, PLAIN_J, :], scalar1=1.0, scalar2=0.0, op0=ALU.mult, op1=ALU.add)
-
-        def prod_u(g, on_v, which=(0, 1)):
-            for i in which:
-                u = cl.tile([P, J, GW], F32, name="u%d" % i, tag="u%d" % i)
-                st["u", g, i] = u
-                eng = nc.vector if on_v else nc.gpsimd
-                for j0 in range(0, J, U_SPLIT):
-                    eng.tensor_tensor(out=u[:, j0 : j0 + U_SPLIT, :], in0=st["x", g, 1 - i][:, j0 : j0 + U_SPLIT, :], in1=st["f", g, i][:, j0 : j0 + U_SPLIT, :], op=ALU.add)
-
-        def where(h):
-            t, i = divmod(h, 2)
-            g, b = divmod(t, 4)
-            return t, i, g, slice(P * b, P * b + P)
-
-        def pe_r(h):
-            t, i, g, cols = where(h)
-            r = ps.tile([P, GW], F32, name="r", tag="r", bufs=R_BUFS)
-            st["r", h] = r
-            for j in (3, 0, 1, 2):
-                o = r[:, P * j : P * j + P]
-                yT = st["y", g, i][:, j, cols]
-                if j == PLAIN_J:
-                    nc.tensor.matmul(o, lhsT=yT, rhs=ident_f[:], is_transpose=True, start=True, stop=False)
-                    nc.tensor.matmul(o, lhsT=st["xf", g][:, i, cols], rhs=ident_f[:], is_transpose=True, start=False, stop=True)
-                elif j == 2 and SANDWICH:
-                    do_m()
-                    nc.tensor.matmul(o, lhsT=st["x", g, 1 - i][:, j, cols], rhs=ident_b[:], start=True, stop=False)
-                    nc.tensor.matmul(o, lhsT=yT, rhs=ident_f[:], is_transpose=True, start=False, stop=True)
-                else:
-                    nc.tensor.matmul(o, lhsT=yT, rhs=ident_f[:], is_transpose=True, start=True, stop=False)
-                    nc.tensor.matmul(o, lhsT=st["x", g, 1 - i][:, j, cols], rhs=ident_b[:], start=False, stop=True)
-
-        def s_a(h):
-            a = wk.tile([P, GW], F32, name="a", tag="a")
-            st["a", h] = a
-            nc.scalar.activation(out=a[:], in_=st["r", h][:], func=ACT.Exp)
-
-        def v_max(h):
-            nm = sm.tile([P, 1], F32, name="nm", tag="nm")
-            st["nm", h] = nm
-            nc.vector.tensor_reduce(out=nm[:], in_=st["a", h][:], axis=AX.X, op=ALU.max, negate=True)
-
-        def s_e(h):
-            t, i, g, cols = where(h)
-            if i == 0:
-                st["se", t] = sm.tile([P, 2], F32, name="se", tag="se")
-            e = wk.tile([P, GW], F32, name="e", tag="e")
-            st["e", h] = e
-            nc.scalar.activation(out=e[:], in_=st["a", h][:], func=ACT.Exp, bias=st["nm", h][:], scale=1.0, accum_out=st["se", t][:, i : i + 1])
-
-        def v_ser(h):
-            t, i, g, cols = where(h)
-            if i == 0:
-                st["ser", t] = sm.tile([P, 2], F32, name="ser", tag="ser")
-            e = st["e", h]
-            nc.vector.scalar_tensor_tensor(out=e[:], in0=e[:], scalar=1.0, in1=st["r", h][:], op0=ALU.mult, op1=ALU.mult, accum_out=st["ser", t][:, i : i + 1])
+                live["sum_er", block] = small.tile([P, 2], F32, name="sum_er", tag="sum_er")
+            e = live["e", h]
+            nc.vector.scalar_tensor_tensor(
+                out=e[:], in0=e[:], scalar=1.0, in1=live["r", h][:], op0=ALU.mult, op1=ALU.mult, accum_out=live["sum_er", block][:, i : i + 1]
+            )
             if i == 1:
-                rse = sm.tile([P, 2], F32, name="rse", tag="rse")
-                s2 = sm.tile([P, 2], F32, name="s2", tag="s2")
-                st["s", t] = s2
-                nc.vector.reciprocal(out=rse[:], in_=st["se", t][:])
-                nc.vector.tensor_tensor(out=s2[:], in0=st["ser", t][:], in1=rse[:], op=ALU.mult)
+                inv = small.tile([P, 2], F32, name="inv", tag="inv")
+                s = small.tile([P, 2], F32, name="s", tag="s")
+                live["s", block] = s
+                nc.vector.reciprocal(out=inv[:], in_=live["sum_e", block][:])
+                nc.vector.tensor_tensor(out=s[:], in0=live["sum_er", block][:], in1=inv[:], op=ALU.mult)
 
-        def pe_x(t):
-            g, b = divmod(t, 4)
+
+        def x_to_positions(block):
+            g, b = divmod(block, 4)
             cols = slice(P * b, P * b + P)
-            x = ps.tile([P, 2, GW], BF16, name="xT", tag="xT", bufs=X_BUFS)
-            st["xT", t] = x
+            xt = psum.tile([P, 2, PACK * P], BF16, name="xt", tag="xt", bufs=1)
+            live["xt", block] = xt
             for i in range(2):
-                for j in range(J):
-                    nc.tensor.transpose(out=x[:, i, P * j : P * j + P], in_=st["x", g, i][:, j, cols], identity=ident_b[:])
+                for j in range(PACK):
+                    nc.tensor.transpose(out=xt[:, i, P * j : P * j + P], in_=live["x", g, i][:, j, cols], identity=ident_b[:])
 
-        def s_t(h):
-            t, i, g, cols = where(h)
-            tt = wk.tile([P, GW], F32, name="tT", tag="tT")
-            st["tT", h] = tt
-            nc.scalar.activation(out=tt[:], in_=st["xT", t][:, i, :], func=ACT.Copy, scale=st["s", t][:, i : i + 1])
+        def scale_x(h):
+            block, i, g, cols = place(h)
+            t = steps.tile([P, PACK * P], F32, name="xs", tag="xs")
+            live["xs", h] = t
+            nc.scalar.activation(out=t[:], in_=live["xt", block][:, i, :], func=ACT.Copy, scale=live["s", block][:, i : i + 1])
 
-        def pe_z(h):
-            z = ps.tile([P, J, P], F32, name="z", tag="z", bufs=Z_BUFS)
-            st["z", h] = z
-            for j in range(J):
-                nc.tensor.transpose(out=z[:, j, :], in_=st["tT", h][:, P * j : P * j + P], identity=ident_f[:])
+        def xs_to_channels(h):
+            z = psum.tile([P, PACK, P], F32, name="z", tag="z", bufs=2)
+            live["z", h] = z
+            for j in range(PACK):
+                nc.tensor.transpose(out=z[:, j, :], in_=live["xs", h][:, P * j : P * j + P], identity=ident_f[:])
 
-        def v_z(h):
-            t, i, g, cols = where(h)
+        def fuse(h):
+            block, i, g, cols = place(h)
             if h % 8 == 0:
-                st["grp", g] = cl.tile([P, 2, GW, J], BF16, name="grp", tag="grp", align_bytes=64)
+                live["re", g] = groups.tile([P, 2, GROUP, PACK], BF16, name="re", tag="re", align_bytes=64)
             nc.vector.tensor_tensor(
-                out=st["grp", g][:, i, cols, :],
-                in0=st["z", h][:].rearrange("p j c -> p c j"),
-                in1=st["u", g, i][:, :, cols].rearrange("p j c -> p c j"),
+                out=live["re", g][:, i, cols, :],
+                in0=live["z", h][:].rearrange("p j c -> p c j"),
+                in1=live["u", g, i][:, :, cols].rearrange("p j c -> p c j"),
                 op=ALU.add,
             )
 
-        def v_q(ch):
-            g, u0, nu = ch
-            if u0 == 0:
-                st["codes", g] = cl.tile([P, 2 * GW], U32, name="codes", tag="codes", align_bytes=64)
-                st["scl", g] = cl.tile([P, 2 * GW], U8, name="scl", tag="scl", align_bytes=64)
-            codes, scl, grp = st["codes", g], st["scl", g], st["grp", g]
-            if nu == 4:
-                nc.vector.quantize_mx(out=codes[:].bitcast(FP8X4), scales=scl[:], in_=grp[:].rearrange("p i c j -> p (i c j)"))
-            else:
-                for s in range(2):
-                    c = slice(GW * s + P * u0, GW * s + P * (u0 + nu))
-                    nc.vector.quantize_mx(
-                        out=codes[:, c].bitcast(FP8X4), scales=scl[:, c],
-                        in_=grp[:, s, P * u0 : P * (u0 + nu), :].rearrange("p c j -> p (c j)"),
-                    )
 
-        def pe_m(ch, m8, tag):
-            g, u0, nu = ch
-            m = ps.tile([P, GW], F32, name="m", tag=tag, bufs=(M_BUFS if tag == "m" else R_BUFS))
-            st["m", ch, m8] = m
-            for d in range(DUMMY):
-                wc = slice(2 * m8 * P, 2 * m8 * P + P)
-                rc = slice(P * u0, P * (u0 + nu))
+        def quantise(g):
+            codes = groups.tile([P, 2 * GROUP], U32, name="codes", tag="codes", align_bytes=64)
+            scales = groups.tile([P, 2 * GROUP], U8, name="scales", tag="scales", align_bytes=64)
+            live["codes", g] = codes
+            live["scales", g] = scales
+            nc.vector.quantize_mx(out=codes[:].bitcast(FP8X4), scales=scales[:], in_=live["re", g][:].rearrange("p i c j -> p (i c j)"))
+
+        def project(q, tag, bufs):
+            g, m = divmod(q, TILES)
+            acc = psum.tile([P, GROUP], F32, name="acc", tag=tag, bufs=bufs)
+            live["acc", q] = acc
+            for i in range(2):
+                wc = slice((2 * m + i) * P, (2 * m + i) * P + P)
+                rc = slice(GROUP * i, GROUP * i + GROUP)
                 nc.tensor.matmul_mx(
-                    out=m[:, 0 : P * nu], lhsT=w_codes[:, wc].bitcast(FP8X4), lhsT_scale=w_scl[:, wc],
-                    rhs=st["codes", g][:, rc].bitcast(FP8X4), rhs_scale=st["scl", g][:, rc],
-                    start=True, stop=True,
-                )
-            for s in range(2):
-                wc = slice((2 * m8 + s) * P, (2 * m8 + s) * P + P)
-                rc = slice(GW * s + P * u0, GW * s + P * (u0 + nu))
-                nc.tensor.matmul_mx(
-                    out=m[:, 0 : P * nu], lhsT=w_codes[:, wc].bitcast(FP8X4), lhsT_scale=w_scl[:, wc],
-                    rhs=st["codes", g][:, rc].bitcast(FP8X4), rhs_scale=st["scl", g][:, rc],
-                    start=(s == 0), stop=(s == 1),
+                    out=acc[:], lhsT=w_codes[:, wc].bitcast(FP8X4), lhsT_scale=w_scales[:, wc],
+                    rhs=live["codes", g][:, rc].bitcast(FP8X4), rhs_scale=live["scales", g][:, rc],
+                    start=(i == 0), stop=(i == 1),
                 )
 
-        def ev_m(ch, m8, on_v):
-            g, u0, nu = ch
-            n, gh = divmod(g, 2)
-            w, mm = divmod(m8, 4)
-            wd = P * nu
-            ob = wk.tile([P, GW], F32, name="ob", tag="ob", bufs=6)
+        def store(q, on_vector):
+            g, m = divmod(q, TILES)
+            n, half = divmod(g, 2)
+            w, mm = divmod(m, 4)
+            o = steps.tile([P, GROUP], F32, name="o", tag="o", bufs=6)
             b = bias[:, mm, w : w + 1]
-            if on_v:
-                nc.vector.tensor_scalar(out=ob[:, 0:wd], in0=st["m", ch, m8][:, 0:wd], scalar1=b, scalar2=None, op0=ALU.add)
+            if on_vector:
+                nc.vector.tensor_scalar(out=o[:], in0=live["acc", q][:], scalar1=b, scalar2=None, op0=ALU.add)
             else:
-                nc.scalar.activation(out=ob[:, 0:wd], in_=st["m", ch, m8][:, 0:wd], func=ACT.Identity, bias=b, scale=1.0)
-            c0 = GW * gh + P * u0
-            nc.sync.dma_start(out=os_[w][n, mm][:, c0 : c0 + wd], in_=ob[:, 0:wd])
+                nc.scalar.activation(out=o[:], in_=live["acc", q][:], func=ACT.Identity, bias=b, scale=1.0)
+            nc.sync.dma_start(out=out_hbm[w][n, mm][:, GROUP * half : GROUP * half + GROUP], in_=o[:])
 
-        gts = []
-        for nm_, src in (("ga", g1), ("gc", g2)):
-            t = const.tile([P, GW], BF16, name=nm_)
+        def w_to_channels(m):
+            w, mm = divmod(m, 4)
+            wt = psum.tile([P, 2, 2, P], F32, name="wt", tag="acc", bufs=2)
+            live["wt", m] = wt
+            words = w_raw[w][:, mm, :].bitcast(F32).rearrange("o (i p u) -> o i u p", i=2, u=2)
+            for i in range(2):
+                for u in range(2):
+                    nc.tensor.transpose(out=wt[:, i, u, :], in_=words[:, i, u, :], identity=ident_f[:])
+
+        def w_quantise(m):
+            w, mm = divmod(m, 4)
+            if mm == 0:
+                live["wg", w] = const.tile([P, 4, 2, P, 2], F32, name="wg", tag="wg", align_bytes=64)
+            src = live["wt", m][:].rearrange("p i u o -> p i o u")
+            if mm % 2 == 0:
+                nc.scalar.copy(out=live["wg", w][:, mm], in_=src)
+            else:
+                nc.vector.tensor_copy(out=live["wg", w][:, mm], in_=src)
+            if mm == 3:
+                c = slice(8 * P * w, 8 * P * w + 8 * P)
+                nc.vector.quantize_mx(
+                    out=w_codes[:, c].bitcast(FP8X4), scales=w_scales[:, c],
+                    in_=live["wg", w][:].rearrange("p m i o u -> p (m i o u)").bitcast(BF16),
+                )
+
+
+        rows = []
+        for name, src, n_rows in (("g1r", g1, 4), ("g2r", g2, 4)):
+            t = const.tile([P, PACK * P], BF16, name=name)
             nc.vector.memset(t[:], 0.0)
-            nc.sync.dma_start(out=t[0:4, :], in_=src)
-            gts.append(t)
+            nc.sync.dma_start(out=t[0:n_rows, :], in_=src)
+            rows.append(t)
         load(0)
-        bts = []
-        for nm_, src in (("ba", p1_b), ("bc", p2_b)):
-            t = const.tile([P, GW], BF16, name=nm_)
+        for name, src in (("b1r", p1_b), ("b2r", p2_b)):
+            t = const.tile([P, PACK * P], BF16, name=name)
             nc.vector.memset(t[:], 0.0)
             nc.sync.dma_start(out=t[0:1, :], in_=src.rearrange("(o c) -> o c", o=1))
-            bts.append(t)
+            rows.append(t)
         ident_b = const.tile([P, P], BF16, name="ident_b")
         make_identity(nc, ident_b[:])
         ident_f = const.tile([P, P], F32, name="ident_f")
@@ -278,162 +236,88 @@ def tile_fr_pb_kernel(tc, x1, x2, FE_x1, FE_x2, g1, g2, p1_w, p1_b, p2_w, p2_b, 
         load(1)
         w_raw = []
         for w in range(2):
-            t = const.tile([P, J, 1024], BF16, name="w_raw%d" % w)
-            nc.sync.dma_start(out=t[:], in_=ws[w])
+            t = const.tile([P, 4, 1024], BF16, name="w_raw%d" % w)
+            nc.sync.dma_start(out=t[:], in_=w_hbm[w])
             w_raw.append(t)
         load(2)
+        w_codes = const.tile([P, 2 * TILES * P], U32, name="w_codes", align_bytes=64)
+        w_scales = const.tile([P, 2 * TILES * P], U8, name="w_scales", align_bytes=64)
 
-        gT = ps.tile([P, 2, J, P], BF16, name="gT", tag="xT", bufs=X_BUFS)
+        g_t = psum.tile([P, 2, PACK, P], BF16, name="g_t", tag="xt", bufs=1)
         for i in range(2):
-            for j in range(J):
-                nc.tensor.transpose(out=gT[:, i, j, :], in_=gts[i][:, P * j : P * j + P], identity=ident_b[:])
-        sg = const.tile([P, J, 8], F32, name="sg")
+            by_j = const.tile([P, PACK, P], BF16, name="by_j%d" % i)
+            nc.vector.tensor_copy(out=by_j[:], in_=rows[i][:].rearrange("r (p j) -> r j p", j=PACK))
+            for j in range(PACK):
+                nc.tensor.transpose(out=g_t[:, i, j, :], in_=by_j[:, j, :], identity=ident_b[:])
+        sig = const.tile([P, PACK, 8], F32, name="sig")
         for i in range(2):
-            nc.scalar.activation(out=sg[:, :, 4 * i : 4 * i + 4], in_=gT[:, i, :, 0:4], func=ACT.Exp, scale=-1.0)
-        nc.vector.tensor_scalar(out=sg[:], in0=sg[:], scalar1=1.0, scalar2=None, op0=ALU.add)
-        nc.vector.reciprocal(out=sg[:], in_=sg[:])
-        bias = const.tile([P, J, 2], F32, name="bias")
+            nc.scalar.activation(out=sig[:, :, 4 * i : 4 * i + 4], in_=g_t[:, i, :, 0:4], func=ACT.Exp, scale=-1.0)
+        nc.vector.tensor_scalar(out=sig[:], in0=sig[:], scalar1=1.0, scalar2=None, op0=ALU.add)
+        nc.vector.reciprocal(out=sig[:], in_=sig[:])
+        bias = const.tile([P, 4, 2], F32, name="bias")
 
-        prod_y(0, True)
-        prod_xf(0)
-        if not Y_V:
-            prod_y(1, False)
+        gate(0, 0)
+        widen(0)
+        gate(0, 1)
+        rest(0)
+        widen(1)
+        rest(1)
+        r_to_positions(0)
 
-        if RAMP_DUMMY:
-            zc = const.tile([P, GW], U32, name="zc", align_bytes=64)
-            zs = const.tile([P, GW], U8, name="zs", align_bytes=64)
-            nc.vector.memset(zc[:].bitcast(mybir.dt.int32), 0)
-            nc.vector.memset(zs[:].bitcast(mybir.dt.int32), 0)
-        w_codes = const.tile([P, 16 * P], U32, name="w_codes", align_bytes=64)
-        w_scl = const.tile([P, 16 * P], U8, name="w_scl", align_bytes=64)
+        for k in range(STEPS + 15):
+            g, phase = divmod(k, 8)
 
-        def w_t(w, mm):
-            wT = ps.tile([P, 8, P], BF16, name="wT", tag="m", bufs=M_BUFS)
-            st["wT", w, mm] = wT
-            for kk in range(8):
-                nc.tensor.transpose(out=wT[:, kk, :], in_=w_raw[w][:, mm, P * kk : P * kk + P], identity=ident_b[:])
+            def due(lag):
+                return 0 <= k - lag < STEPS
 
-        def w_ev(w, mm):
-            if mm == 0:
-                st["wg", w] = const.tile([P, J, 2, P, 4], BF16, name="wg", tag="wg", align_bytes=64)
-            src = st["wT", w, mm][:].rearrange("p (s t) o -> p s o t", t=4)
-            if mm % 2 == 0:
-                nc.scalar.copy(out=st["wg", w][:, mm], in_=src)
-            else:
-                nc.vector.tensor_copy(out=st["wg", w][:, mm], in_=src)
-            if mm == 3:
-                c = slice(1024 * w, 1024 * w + 1024)
-                nc.vector.quantize_mx(out=w_codes[:, c].bitcast(FP8X4), scales=w_scl[:, c], in_=st["wg", w][:].rearrange("p m s o t -> p (m s o t)"))
-
-        chunks = [(g, 0, 4) for g in range(NG - 1)] + [(NG - 1, u0, nu) for (u0, nu) in LAST]
-        cnt = {"z": 0, "q": 0, "done": 0, "evd": 0, "k": 0, "avail": 0}
-        jobs = []
-        istep = []
-
-        def on(h):
-            return 0 <= h < NH
-
-        def do_q():
-            if cnt["q"] < len(chunks):
-                ch = chunks[cnt["q"]]
-                if cnt["z"] >= 8 * ch[0] + 2 * (ch[1] + ch[2]):
-                    v_q(ch)
-                    jobs.extend([(ch, m8) for m8 in range(8)])
-                    cnt["q"] += 1
-
-        def do_m():
-            if cnt["k"] < NH and cnt["k"] % MX_EVERY != 0:
-                return
-            for rep2 in range(MX_EVERY if cnt["k"] < NH else 1):
-                do_m1()
-
-        def do_m1():
-            if cnt["done"] >= cnt["avail"] and cnt["q"] == 0 and RAMP_DUMMY:
-                m = ps.tile([P, GW], F32, name="m", tag="m", bufs=M_BUFS)
-                for d in range(RAMP_DUMMY):
-                    nc.tensor.matmul_mx(
-                        out=m[:], lhsT=zc[:, 0:P].bitcast(FP8X4), lhsT_scale=zs[:, 0:P],
-                        rhs=zc[:].bitcast(FP8X4), rhs_scale=zs[:], start=True, stop=True,
-                    )
-            if cnt["done"] < cnt["avail"]:
-                tail = cnt["k"] >= NH
-                pe_m(jobs[cnt["done"]][0], jobs[cnt["done"]][1], TAIL_TAGS[cnt["done"] % len(TAIL_TAGS)] if tail else "m")
-                istep.append(cnt["k"])
-                cnt["done"] += 1
-
-        def do_ev(k):
-            e = cnt["evd"]
-            lag = 1 if k < NH + 1 else TAIL_LAG
-            if e < cnt["done"] - lag or (e < cnt["done"] and (cnt["done"] == len(jobs) or istep[e] < k)):
-                ev_m(jobs[e][0], jobs[e][1], (jobs[e][1] in V_EV) if k < NH else (e % 2 == 1))
-                cnt["evd"] += 1
-
-        def misc(k):
+            if due(0):
+                exp_r(k)
+            if due(1):
+                exp_shifted(k - 1)
+            if due(6):
+                fuse(k - 6)
+            if due(0):
+                neg_max(k)
+            if due(1):
+                weigh(k - 1)
+            if due(4):
+                scale_x(k - 4)
+            if 4 <= k < 4 + TILES:
+                w_quantise(k - 4)
+            if due(5):
+                xs_to_channels(k - 5)
+            if due(-1):
+                r_to_positions(k + 1)
+            q = k - 14
+            late = k >= STEPS
+            if 0 <= q < GROUPS * TILES:
+                if late and q % 2 == 1:
+                    project(q, "r", 3)
+                else:
+                    project(q, "acc", 2)
+            if 0 <= q - 1 < GROUPS * TILES:
+                store(q - 1, late and q % 2 == 1)
+            if phase == 5 and 1 <= g <= GROUPS:
+                quantise(g - 1)
+            if due(3) and (k - 3) % 2 == 0:
+                x_to_positions((k - 3) // 2)
+            if 3 <= k < 3 + TILES:
+                w_to_channels(k - 3)
             if k == 2:
-                bT = ps.tile([P, 2, J, P], BF16, name="bT", tag="m", bufs=M_BUFS)
+                b_t = psum.tile([P, 2, 4, P], BF16, name="b_t", tag="acc", bufs=2)
                 for w in range(2):
-                    for j in range(J):
-                        nc.tensor.transpose(out=bT[:, w, j, :], in_=bts[w][:, P * j : P * j + P], identity=ident_b[:])
+                    for mm in range(4):
+                        nc.tensor.transpose(out=b_t[:, w, mm, :], in_=rows[2 + w][:, P * mm : P * mm + P], identity=ident_b[:])
                 for w in range(2):
-                    nc.vector.tensor_copy(out=bias[:, :, w : w + 1], in_=bT[:, w, :, 0:1])
-            if k in (1, 2):
-                prod_u(0, True, (k - 1,))
-            if k == 2:
-                prod_u(1, False)
-            gk, rk = divmod(k, 8)
-            if Y_V:
-                if gk + 1 < NG:
-                    y_piece(gk + 1, rk)
-                    if rk in (2, 5):
-                        xf_piece(gk + 1, rk // 4)
-            else:
-                if rk == Y_STEP and 2 <= gk + 1 < NG:
-                    prod_y(gk + 1, False)
-                if rk == XF_STEP and gk + 1 < NG:
-                    prod_xf(gk + 1)
-            if rk == U_STEP and 2 <= gk + 1 < NG:
-                prod_u(gk + 1, False)
-            if rk == LD_STEP and gk + 3 < NG:
-                load(gk + 3)
-
-        simple = {"v_ser": v_ser, "s_a": s_a, "s_e": s_e, "v_max": v_max, "s_t": s_t, "pe_r": pe_r, "pe_z": pe_z}
-        lag_r = [lag for (nm_, lag) in ORDER if nm_ == "pe_r"][0]
-        lag_x = [lag for (nm_, lag) in ORDER if nm_ == "pe_x"][0]
-        for h in range(-lag_r):
-            pe_r(h)
-        k = 0
-        while cnt["evd"] < 8 * len(chunks):
-            cnt["avail"] = len(jobs)
-            cnt["k"] = k
-            for rep in range(1 if k < NH else (MID_RATE if k < NH + TAIL_AT else TAIL_RATE)):
-                for (nm_, lag) in ORDER:
-                    h = k - lag
-                    if nm_ == "pe_m":
-                        if not (SANDWICH and on(k - lag_r)):
-                            do_m()
-                    elif nm_ == "ev_m":
-                        do_ev(k)
-                    elif rep > 0:
-                        continue
-                    elif nm_ in simple:
-                        if on(h):
-                            simple[nm_](h)
-                    elif nm_ == "v_z":
-                        if on(h):
-                            v_z(h)
-                            cnt["z"] += 1
-                    elif nm_ == "v_q":
-                        do_q()
-                    elif nm_ == "pe_x":
-                        if h % 2 == 0 and on(h):
-                            pe_x(h // 2)
-                    elif nm_ == "w_t":
-                        if W0 <= k < W0 + 8:
-                            w_t((k - W0) // 4, (k - W0) % 4)
-                    elif nm_ == "w_ev":
-                        if W0 < k <= W0 + 8:
-                            w_ev((k - W0 - 1) // 4, (k - W0 - 1) % 4)
-                    elif nm_ == "misc":
-                        misc(k)
-                cnt["avail"] = len(jobs)
-            k += 1
+                    nc.vector.tensor_copy(out=bias[:, :, w : w + 1], in_=b_t[:, w, :, 0:1])
+            if g + 1 < GROUPS:
+                if phase == 1:
+                    gate(g + 1, 0)
+                if phase == 5:
+                    gate(g + 1, 1)
+                if phase == 3 and g >= 1:
+                    widen(g + 1)
+                if phase == 7 and g >= 1:
+                    rest(g + 1)
+            if phase == 6 and g + 3 < GROUPS:
+                load(g + 3)

@@ -55,27 +55,25 @@ def tile_fr_pb_kernel(tc, x1, x2, FE_x1, FE_x2, g1, g2, p1_w, p1_b, p2_w, p2_b, 
                     nc.sync.dma_start(out=t[:], in_=hbm[i][n][:, :, cols])
                     live[kind, g, i] = t
 
-        def gate(g, i):
+        def gate(g, piece):
             n = g // 2
-            y = groups.tile([P, PACK, GROUP], F32, name="y%d" % i, tag="y%d" % i)
-            live["y", g, i] = y
-            for j in range(PACK):
-                nc.vector.tensor_scalar(
-                    out=y[:, j, :], in0=live["x", g, i][:, j, :], scalar1=sig[:, j, 4 * i + n : 4 * i + n + 1], scalar2=None, op0=ALU.mult
-                )
+            i, j = divmod(piece, PACK)
+            if j == 0:
+                live["y", g, i] = groups.tile([P, PACK, GROUP], F32, name="y%d" % i, tag="y%d" % i)
+            y, x, s = live["y", g, i][:, j, :], live["x", g, i][:, j, :], sig[:, j, 4 * i + n : 4 * i + n + 1]
+            if j < PLAIN:
+                nc.scalar.activation(out=y, in_=x, func=ACT.Copy, scale=s)
+            else:
+                nc.vector.tensor_scalar(out=y, in0=x, scalar1=s, scalar2=None, op0=ALU.mult)
+                if i == 0:
+                    live["xf", g] = groups.tile([P, 2, GROUP], F32, name="xf", tag="xf")
+                nc.vector.tensor_copy(out=live["xf", g][:, i, :], in_=live["x", g, 1 - i][:, PLAIN, :])
 
-        def widen(g):
-            xf = groups.tile([P, 2, GROUP], F32, name="xf", tag="xf")
-            live["xf", g] = xf
-            for i in range(2):
-                nc.gpsimd.tensor_scalar(out=xf[:, i, :], in0=live["x", g, 1 - i][:, PLAIN, :], scalar1=1.0, scalar2=0.0, op0=ALU.mult, op1=ALU.add)
-
-        def rest(g):
-            for i in range(2):
-                u = groups.tile([P, PACK, GROUP], F32, name="u%d" % i, tag="u%d" % i)
-                live["u", g, i] = u
-                for j in range(PACK):
-                    nc.gpsimd.tensor_tensor(out=u[:, j, :], in0=live["x", g, 1 - i][:, j, :], in1=live["fe", g, i][:, j, :], op=ALU.add)
+        def rest(g, piece):
+            i, j = divmod(piece, PACK)
+            if j == 0:
+                live["u", g, i] = groups.tile([P, PACK, GROUP], F32, name="u%d" % i, tag="u%d" % i)
+            nc.vector.tensor_tensor(out=live["u", g, i][:, j, :], in0=live["x", g, 1 - i][:, j, :], in1=live["fe", g, i][:, j, :], op=ALU.add)
 
 
         def r_to_positions(h):
@@ -256,15 +254,8 @@ def tile_fr_pb_kernel(tc, x1, x2, FE_x1, FE_x2, g1, g2, p1_w, p1_b, p2_w, p2_b, 
         nc.vector.reciprocal(out=sig[:], in_=sig[:])
         bias = const.tile([P, 4, 2], F32, name="bias")
 
-        gate(0, 0)
-        widen(0)
-        gate(0, 1)
-        rest(0)
-        widen(1)
-        rest(1)
-        r_to_positions(0)
 
-        for k in range(STEPS + 15):
+        for k in range(-9, STEPS + 15):
             g, phase = divmod(k, 8)
 
             def due(lag):
@@ -310,14 +301,9 @@ def tile_fr_pb_kernel(tc, x1, x2, FE_x1, FE_x2, g1, g2, p1_w, p1_b, p2_w, p2_b, 
                         nc.tensor.transpose(out=b_t[:, w, mm, :], in_=rows[2 + w][:, P * mm : P * mm + P], identity=ident_b[:])
                 for w in range(2):
                     nc.vector.tensor_copy(out=bias[:, :, w : w + 1], in_=b_t[:, w, :, 0:1])
-            if g + 1 < GROUPS:
-                if phase == 1:
-                    gate(g + 1, 0)
-                if phase == 5:
-                    gate(g + 1, 1)
-                if phase == 3 and g >= 1:
-                    widen(g + 1)
-                if phase == 7 and g >= 1:
-                    rest(g + 1)
-            if phase == 6 and g + 3 < GROUPS:
+            if 0 <= (k + 9) // 8 < GROUPS:
+                gate((k + 9) // 8, (k + 9) % 8)
+            if 0 <= (k + 2) // 8 < GROUPS:
+                rest((k + 2) // 8, (k + 2) % 8)
+            if phase == 6 and 0 <= g and g + 3 < GROUPS:
                 load(g + 3)

@@ -20,7 +20,7 @@ GROUP = 512
 STEPS = 64
 GROUPS = 8
 TILES = 8
-PLAIN = 3
+PLAIN = 2
 
 
 def tile_fr_pb_kernel(tc, x1, x2, FE_x1, FE_x2, g1, g2, p1_w, p1_b, p2_w, p2_b, out_0, out_1):
@@ -64,29 +64,28 @@ def tile_fr_pb_kernel(tc, x1, x2, FE_x1, FE_x2, g1, g2, p1_w, p1_b, p2_w, p2_b, 
             if j < PLAIN:
                 nc.scalar.activation(out=y, in_=x, func=ACT.Copy, scale=s)
             else:
-                nc.vector.tensor_scalar(out=y, in0=x, scalar1=s, scalar2=None, op0=ALU.mult)
-                if i == 0:
-                    live["xf", g] = groups.tile([P, 2, GROUP], F32, name="xf", tag="xf")
-                nc.vector.tensor_copy(out=live["xf", g][:, i, :], in_=live["x", g, 1 - i][:, PLAIN, :])
+                nc.vector.scalar_tensor_tensor(out=y, in0=x, scalar=s, in1=live["x", g, 1 - i][:, j, :], op0=ALU.mult, op1=ALU.add)
 
         def rest(g, piece):
             i, j = divmod(piece, PACK)
             if j == 0:
                 live["u", g, i] = groups.tile([P, PACK, GROUP], F32, name="u%d" % i, tag="u%d" % i)
-            nc.vector.tensor_tensor(out=live["u", g, i][:, j, :], in0=live["x", g, 1 - i][:, j, :], in1=live["fe", g, i][:, j, :], op=ALU.add)
+            nc.gpsimd.tensor_tensor(out=live["u", g, i][:, j, :], in0=live["x", g, 1 - i][:, j, :], in1=live["fe", g, i][:, j, :], op=ALU.add)
 
 
-        def r_to_positions(h):
+        def r_to_positions(h, q):
             block, i, g, cols = place(h)
             r = psum.tile([P, PACK * P], F32, name="r", tag="r", bufs=3)
             live["r", h] = r
-            for j in (PLAIN, 0, 1, 2):
-                o = r[:, P * j : P * j + P]
-                nc.tensor.matmul(o, lhsT=live["y", g, i][:, j, cols], rhs=ident_f[:], is_transpose=True, start=True, stop=False)
-                if j < PLAIN:
-                    nc.tensor.matmul(o, lhsT=live["x", g, 1 - i][:, j, cols], rhs=ident_b[:], start=False, stop=True)
-                else:
-                    nc.tensor.matmul(o, lhsT=live["xf", g][:, i, cols], rhs=ident_f[:], is_transpose=True, start=False, stop=True)
+            y, xj = live["y", g, i], live["x", g, 1 - i]
+            for j in range(PLAIN, PACK):
+                nc.tensor.transpose(out=r[:, P * j : P * j + P], in_=y[:, j, cols], identity=ident_f[:])
+            nc.tensor.matmul(r[:, 0:P], lhsT=y[:, 0, cols], rhs=ident_f[:], is_transpose=True, start=True, stop=False)
+            nc.tensor.matmul(r[:, 0:P], lhsT=xj[:, 0, cols], rhs=ident_b[:], start=False, stop=True)
+            if 0 <= q < GROUPS * TILES:
+                project(q, "acc", 2)
+            nc.tensor.matmul(r[:, P : 2 * P], lhsT=xj[:, 1, cols], rhs=ident_b[:], start=True, stop=False)
+            nc.tensor.matmul(r[:, P : 2 * P], lhsT=y[:, 1, cols], rhs=ident_f[:], is_transpose=True, start=False, stop=True)
 
         def exp_r(h):
             a = steps.tile([P, PACK * P], F32, name="a", tag="a")
@@ -277,17 +276,17 @@ def tile_fr_pb_kernel(tc, x1, x2, FE_x1, FE_x2, g1, g2, p1_w, p1_b, p2_w, p2_b, 
                 w_quantise(k - 4)
             if due(5):
                 xs_to_channels(k - 5)
-            if due(-1):
-                r_to_positions(k + 1)
             q = k - 14
             late = k >= STEPS
-            if 0 <= q < GROUPS * TILES:
+            if due(-1):
+                r_to_positions(k + 1, q)
+            elif 0 <= q < GROUPS * TILES:
                 if late and q % 2 == 1:
                     project(q, "r", 3)
                 else:
                     project(q, "acc", 2)
             if 0 <= q - 1 < GROUPS * TILES:
-                store(q - 1, late and q % 2 == 1)
+                store(q - 1, q % 2 == 1 if late else q % 4 == 0)
             if phase == 5 and 1 <= g <= GROUPS:
                 quantise(g - 1)
             if due(3) and (k - 3) % 2 == 0:

@@ -82,10 +82,10 @@ def tile_fr_pb_kernel(tc, x1, x2, FE_x1, FE_x2, g1, g2, p1_w, p1_b, p2_w, p2_b, 
                 nc.tensor.transpose(out=r[:, P * j : P * j + P], in_=y[:, j, cols], identity=ident_f[:])
             nc.tensor.matmul(r[:, 0:P], lhsT=y[:, 0, cols], rhs=ident_f[:], is_transpose=True, start=True, stop=False)
             nc.tensor.matmul(r[:, 0:P], lhsT=xj[:, 0, cols], rhs=ident_b[:], start=False, stop=True)
-            if 0 <= q < GROUPS * TILES:
-                project(q, "acc", 2)
             nc.tensor.matmul(r[:, P : 2 * P], lhsT=xj[:, 1, cols], rhs=ident_b[:], start=True, stop=False)
             nc.tensor.matmul(r[:, P : 2 * P], lhsT=y[:, 1, cols], rhs=ident_f[:], is_transpose=True, start=False, stop=True)
+            if 0 <= q < GROUPS * TILES:
+                project(q, "acc", 2)
 
         def exp_r(h):
             a = steps.tile([P, PACK * P], F32, name="a", tag="a")

@@ -62,7 +62,7 @@ def tile_fr_pb_kernel(tc, x1, x2, FE_x1, FE_x2, g1, g2, p1_w, p1_b, p2_w, p2_b, 
                 live["y", g, i] = groups.tile([P, PACK, GROUP], F32, name="y%d" % i, tag="y%d" % i)
             y, x, s = live["y", g, i][:, j, :], live["x", g, i][:, j, :], sig[:, j, 4 * i + n : 4 * i + n + 1]
             if j < PLAIN:
-                nc.scalar.activation(out=y, in_=x, func=ACT.Copy, scale=s)
+                nc.gpsimd.tensor_scalar(out=y, in0=x, scalar1=s, scalar2=0.0, op0=ALU.mult, op1=ALU.add)
             else:
                 nc.vector.scalar_tensor_tensor(out=y, in0=x, scalar=s, in1=live["x", g, 1 - i][:, j, :], op0=ALU.mult, op1=ALU.add)
 
@@ -286,7 +286,7 @@ def tile_fr_pb_kernel(tc, x1, x2, FE_x1, FE_x2, g1, g2, p1_w, p1_b, p2_w, p2_b, 
                 else:
                     project(q, "acc", 2)
             if 0 <= q - 1 < GROUPS * TILES:
-                store(q - 1, q % 2 == 1 if late else q % 4 == 0)
+                store(q - 1, q % 2 == 1 if late else False)
             if phase == 5 and 1 <= g <= GROUPS:
                 quantise(g - 1)
             if due(3) and (k - 3) % 2 == 0:

@@ -20,7 +20,7 @@ GROUP = 512
 STEPS = 64
 GROUPS = 8
 TILES = 8
-PLAIN = 2
+PLAIN = 3
 
 
 def tile_fr_pb_kernel(tc, x1, x2, FE_x1, FE_x2, g1, g2, p1_w, p1_b, p2_w, p2_b, out_0, out_1):
@@ -61,10 +61,19 @@ def tile_fr_pb_kernel(tc, x1, x2, FE_x1, FE_x2, g1, g2, p1_w, p1_b, p2_w, p2_b, 
             if j == 0:
                 live["y", g, i] = groups.tile([P, PACK, GROUP], F32, name="y%d" % i, tag="y%d" % i)
             y, x, s = live["y", g, i][:, j, :], live["x", g, i][:, j, :], sig[:, j, 4 * i + n : 4 * i + n + 1]
-            if j < PLAIN:
+            if g > 0:
                 nc.gpsimd.tensor_scalar(out=y, in0=x, scalar1=s, scalar2=0.0, op0=ALU.mult, op1=ALU.add)
+            elif j % 2 == 0:
+                nc.scalar.activation(out=y, in_=x, func=ACT.Copy, scale=s)
             else:
-                nc.vector.scalar_tensor_tensor(out=y, in0=x, scalar=s, in1=live["x", g, 1 - i][:, j, :], op0=ALU.mult, op1=ALU.add)
+                nc.vector.tensor_scalar(out=y, in0=x, scalar1=s, scalar2=None, op0=ALU.mult)
+            if j >= PLAIN:
+                xf = groups.tile([P, GROUP], F32, name="xf%d" % i, tag="xf%d" % i)
+                live["xf", g, i] = xf
+                if g > 0:
+                    nc.gpsimd.tensor_scalar(out=xf[:], in0=live["x", g, 1 - i][:, j, :], scalar1=1.0, scalar2=0.0, op0=ALU.mult, op1=ALU.add)
+                else:
+                    nc.vector.tensor_copy(out=xf[:], in_=live["x", g, 1 - i][:, j, :])
 
         def rest(g, piece):
             i, j = divmod(piece, PACK)
@@ -78,12 +87,14 @@ def tile_fr_pb_kernel(tc, x1, x2, FE_x1, FE_x2, g1, g2, p1_w, p1_b, p2_w, p2_b, 
             r = psum.tile([P, PACK * P], F32, name="r", tag="r", bufs=3)
             live["r", h] = r
             y, xj = live["y", g, i], live["x", g, 1 - i]
-            for j in range(PLAIN, PACK):
-                nc.tensor.transpose(out=r[:, P * j : P * j + P], in_=y[:, j, cols], identity=ident_f[:])
-            nc.tensor.matmul(r[:, 0:P], lhsT=y[:, 0, cols], rhs=ident_f[:], is_transpose=True, start=True, stop=False)
-            nc.tensor.matmul(r[:, 0:P], lhsT=xj[:, 0, cols], rhs=ident_b[:], start=False, stop=True)
+            nc.tensor.matmul(r[:, 3 * P : 4 * P], lhsT=live["xf", g, i][:, cols], rhs=ident_f[:], is_transpose=True, start=True, stop=False)
+            nc.tensor.matmul(r[:, 3 * P : 4 * P], lhsT=y[:, 3, cols], rhs=ident_f[:], is_transpose=True, start=False, stop=True)
+            nc.tensor.matmul(r[:, 2 * P : 3 * P], lhsT=y[:, 2, cols], rhs=ident_f[:], is_transpose=True, start=True, stop=False)
+            nc.tensor.matmul(r[:, 2 * P : 3 * P], lhsT=xj[:, 2, cols], rhs=ident_b[:], start=False, stop=True)
             nc.tensor.matmul(r[:, P : 2 * P], lhsT=xj[:, 1, cols], rhs=ident_b[:], start=True, stop=False)
             nc.tensor.matmul(r[:, P : 2 * P], lhsT=y[:, 1, cols], rhs=ident_f[:], is_transpose=True, start=False, stop=True)
+            nc.tensor.matmul(r[:, 0:P], lhsT=y[:, 0, cols], rhs=ident_f[:], is_transpose=True, start=True, stop=False)
+            nc.tensor.matmul(r[:, 0:P], lhsT=xj[:, 0, cols], rhs=ident_b[:], start=False, stop=True)
             if 0 <= q < GROUPS * TILES:
                 project(q, "acc", 2)
 
@@ -117,10 +128,13 @@ def tile_fr_pb_kernel(tc, x1, x2, FE_x1, FE_x2, g1, g2, p1_w, p1_b, p2_w, p2_b, 
             )
             if i == 1:
                 inv = small.tile([P, 2], F32, name="inv", tag="inv")
-                s = small.tile([P, 2], F32, name="s", tag="s")
-                live["s", block] = s
+                live["inv", block] = inv
                 nc.vector.reciprocal(out=inv[:], in_=live["sum_e", block][:])
-                nc.vector.tensor_tensor(out=s[:], in0=live["sum_er", block][:], in1=inv[:], op=ALU.mult)
+
+        def divide(block):
+            s = small.tile([P, 2], F32, name="s", tag="s")
+            live["s", block] = s
+            nc.gpsimd.tensor_tensor(out=s[:], in0=live["sum_er", block][:], in1=live["inv", block][:], op=ALU.mult)
 
 
         def x_to_positions(block):
@@ -286,7 +300,7 @@ def tile_fr_pb_kernel(tc, x1, x2, FE_x1, FE_x2, g1, g2, p1_w, p1_b, p2_w, p2_b, 
                 else:
                     project(q, "acc", 2)
             if 0 <= q - 1 < GROUPS * TILES:
-                store(q - 1, q % 2 == 1 if late else False)
+                store(q - 1, q % 2 == 1 if late else q % 4 == 0)
             if phase == 5 and 1 <= g <= GROUPS:
                 quantise(g - 1)
             if due(3) and (k - 3) % 2 == 0:
@@ -304,5 +318,7 @@ def tile_fr_pb_kernel(tc, x1, x2, FE_x1, FE_x2, g1, g2, p1_w, p1_b, p2_w, p2_b, 
                 gate((k + 9) // 8, (k + 9) % 8)
             if 0 <= (k + 2) // 8 < GROUPS:
                 rest((k + 2) // 8, (k + 2) % 8)
+            if due(1) and (k - 1) % 2 == 1:
+                divide((k - 1) // 2)
             if phase == 6 and 0 <= g and g + 3 < GROUPS:
                 load(g + 3)

@@ -61,9 +61,9 @@ def tile_fr_pb_kernel(tc, x1, x2, FE_x1, FE_x2, g1, g2, p1_w, p1_b, p2_w, p2_b, 
             if j == 0:
                 live["y", g, i] = groups.tile([P, PACK, GROUP], F32, name="y%d" % i, tag="y%d" % i)
             y, x, s = live["y", g, i][:, j, :], live["x", g, i][:, j, :], sig[:, j, 4 * i + n : 4 * i + n + 1]
-            if g > 0:
+            if g > 0 and j >= 2:
                 nc.gpsimd.tensor_scalar(out=y, in0=x, scalar1=s, scalar2=0.0, op0=ALU.mult, op1=ALU.add)
-            elif j % 2 == 0:
+            elif g > 0 or j % 2 == 0:
                 nc.scalar.activation(out=y, in_=x, func=ACT.Copy, scale=s)
             else:
                 nc.vector.tensor_scalar(out=y, in0=x, scalar1=s, scalar2=None, op0=ALU.mult)
@@ -71,7 +71,7 @@ def tile_fr_pb_kernel(tc, x1, x2, FE_x1, FE_x2, g1, g2, p1_w, p1_b, p2_w, p2_b, 
                 xf = groups.tile([P, GROUP], F32, name="xf%d" % i, tag="xf%d" % i)
                 live["xf", g, i] = xf
                 if g > 0:
-                    nc.gpsimd.tensor_scalar(out=xf[:], in0=live["x", g, 1 - i][:, j, :], scalar1=1.0, scalar2=0.0, op0=ALU.mult, op1=ALU.add)
+                    nc.scalar.copy(out=xf[:], in_=live["x", g, 1 - i][:, j, :])
                 else:
                     nc.vector.tensor_copy(out=xf[:], in_=live["x", g, 1 - i][:, j, :])
 
@@ -131,10 +131,13 @@ def tile_fr_pb_kernel(tc, x1, x2, FE_x1, FE_x2, g1, g2, p1_w, p1_b, p2_w, p2_b, 
                 live["inv", block] = inv
                 nc.vector.reciprocal(out=inv[:], in_=live["sum_e", block][:])
 
-        def divide(block):
-            s = small.tile([P, 2], F32, name="s", tag="s")
-            live["s", block] = s
-            nc.gpsimd.tensor_tensor(out=s[:], in0=live["sum_er", block][:], in1=live["inv", block][:], op=ALU.mult)
+        def divide(h):
+            block, i, g, cols = place(h)
+            if i == 0:
+                live["s", block] = small.tile([P, 2], F32, name="s", tag="s")
+            nc.scalar.activation(
+                out=live["s", block][:, i : i + 1], in_=live["sum_er", block][:, i : i + 1], func=ACT.Copy, scale=live["inv", block][:, i : i + 1]
+            )
 
 
         def x_to_positions(block):
@@ -284,6 +287,8 @@ def tile_fr_pb_kernel(tc, x1, x2, FE_x1, FE_x2, g1, g2, p1_w, p1_b, p2_w, p2_b, 
                 neg_max(k)
             if due(1):
                 weigh(k - 1)
+            if due(3):
+                divide(k - 3)
             if due(4):
                 scale_x(k - 4)
             if 4 <= k < 4 + TILES:
@@ -300,7 +305,7 @@ def tile_fr_pb_kernel(tc, x1, x2, FE_x1, FE_x2, g1, g2, p1_w, p1_b, p2_w, p2_b, 
                 else:
                     project(q, "acc", 2)
             if 0 <= q - 1 < GROUPS * TILES:
-                store(q - 1, q % 2 == 1 if late else q % 4 == 0)
+                store(q - 1, q % 2 == 1 if late else q % 8 not in (1, 4, 7))
             if phase == 5 and 1 <= g <= GROUPS:
                 quantise(g - 1)
             if due(3) and (k - 3) % 2 == 0:
@@ -318,7 +323,5 @@ def tile_fr_pb_kernel(tc, x1, x2, FE_x1, FE_x2, g1, g2, p1_w, p1_b, p2_w, p2_b, 
                 gate((k + 9) // 8, (k + 9) % 8)
             if 0 <= (k + 2) // 8 < GROUPS:
                 rest((k + 2) // 8, (k + 2) % 8)
-            if due(1) and (k - 1) % 2 == 1:
-                divide((k - 1) // 2)
             if phase == 6 and 0 <= g and g + 3 < GROUPS:
                 load(g + 3)

@@ -88,13 +88,10 @@ def tile_fr_pb_kernel(tc, x1, x2, FE_x1, FE_x2, g1, g2, p1_w, p1_b, p2_w, p2_b, 
             live["r", h] = r
             y, xj = live["y", g, i], live["x", g, 1 - i]
             nc.tensor.matmul(r[:, 3 * P : 4 * P], lhsT=live["xf", g, i][:, cols], rhs=ident_f[:], is_transpose=True, start=True, stop=False)
-            nc.tensor.matmul(r[:, 3 * P : 4 * P], lhsT=y[:, 3, cols], rhs=ident_f[:], is_transpose=True, start=False, stop=True)
-            nc.tensor.matmul(r[:, 2 * P : 3 * P], lhsT=y[:, 2, cols], rhs=ident_f[:], is_transpose=True, start=True, stop=False)
-            nc.tensor.matmul(r[:, 2 * P : 3 * P], lhsT=xj[:, 2, cols], rhs=ident_b[:], start=False, stop=True)
-            nc.tensor.matmul(r[:, P : 2 * P], lhsT=xj[:, 1, cols], rhs=ident_b[:], start=True, stop=False)
-            nc.tensor.matmul(r[:, P : 2 * P], lhsT=y[:, 1, cols], rhs=ident_f[:], is_transpose=True, start=False, stop=True)
-            nc.tensor.matmul(r[:, 0:P], lhsT=y[:, 0, cols], rhs=ident_f[:], is_transpose=True, start=True, stop=False)
-            nc.tensor.matmul(r[:, 0:P], lhsT=xj[:, 0, cols], rhs=ident_b[:], start=False, stop=True)
+            for j in (3, 2, 1, 0):
+                nc.tensor.matmul(r[:, j * P : j * P + P], lhsT=y[:, j, cols], rhs=ident_f[:], is_transpose=True, start=False, stop=False)
+            for j in (2, 1, 0):
+                nc.tensor.matmul(r[:, j * P : j * P + P], lhsT=xj[:, j, cols], rhs=ident_b[:], start=False, stop=(j == 0))
             if 0 <= q < GROUPS * TILES:
                 project(q, "acc", 2)
 

@@ -305,6 +305,8 @@ def tile_fr_pb_kernel(tc, x1, x2, FE_x1, FE_x2, g1, g2, p1_w, p1_b, p2_w, p2_b, 
                 store(q - 1, q % 2 == 1 if late else q % 8 not in (1, 4, 7))
             if phase == 5 and 1 <= g <= GROUPS:
                 quantise(g - 1)
+                hold = small.tile([P, 1], F32, name="hold", tag="hold")
+                nc.vector.tensor_copy(out=hold[:], in_=live["u", g - 1, 0][:, 0, 0:1])
             if due(3) and (k - 3) % 2 == 0:
                 x_to_positions((k - 3) // 2)
             if 3 <= k < 3 + TILES:

@@ -20,7 +20,10 @@ GROUP = 512
 STEPS = 64
 GROUPS = 8
 TILES = 8
-PLAIN = 3
+
+
+def by_matmul(h):
+    return h % 4 != 3
 
 
 def tile_fr_pb_kernel(tc, x1, x2, FE_x1, FE_x2, g1, g2, p1_w, p1_b, p2_w, p2_b, out_0, out_1):
@@ -46,52 +49,46 @@ def tile_fr_pb_kernel(tc, x1, x2, FE_x1, FE_x2, g1, g2, p1_w, p1_b, p2_w, p2_b, 
             return block, i, g, slice(P * b, P * b + P)
 
 
-        def load(g):
+        def load(kind, g):
             n, half = divmod(g, 2)
             cols = slice(GROUP * half, GROUP * half + GROUP)
-            for kind, hbm, bufs in (("x", x_hbm, 4), ("fe", fe_hbm, 3)):
-                for i in range(2):
-                    t = groups.tile([P, PACK, GROUP], BF16, name="%s%d" % (kind, i), tag="%s%d" % (kind, i), bufs=bufs)
-                    nc.sync.dma_start(out=t[:], in_=hbm[i][n][:, :, cols])
-                    live[kind, g, i] = t
+            hbm, bufs = {"x": (x_hbm, 4), "fe": (fe_hbm, 3)}[kind]
+            for i in range(2):
+                t = groups.tile([P, PACK, GROUP], BF16, name="%s%d" % (kind, i), tag="%s%d" % (kind, i), bufs=bufs)
+                nc.sync.dma_start(out=t[:], in_=hbm[i][n][:, :, cols])
+                live[kind, g, i] = t
 
         def gate(g, piece):
             n = g // 2
             i, j = divmod(piece, PACK)
             if j == 0:
                 live["y", g, i] = groups.tile([P, PACK, GROUP], F32, name="y%d" % i, tag="y%d" % i)
+                live["xf", g, i] = groups.tile([P, PACK, GROUP], F32, name="xf%d" % i, tag="xf%d" % i)
             y, x, s = live["y", g, i][:, j, :], live["x", g, i][:, j, :], sig[:, j, 4 * i + n : 4 * i + n + 1]
-            if g > 0 and j >= 2:
+            xf, xj = live["xf", g, i][:, j, :], live["x", g, 1 - i][:, j, :]
+            if g > 0:
                 nc.gpsimd.tensor_scalar(out=y, in0=x, scalar1=s, scalar2=0.0, op0=ALU.mult, op1=ALU.add)
-            elif g > 0 or j % 2 == 0:
-                nc.scalar.activation(out=y, in_=x, func=ACT.Copy, scale=s)
+                nc.gpsimd.tensor_scalar(out=xf, in0=xj, scalar1=1.0, scalar2=0.0, op0=ALU.mult, op1=ALU.add)
             else:
-                nc.vector.tensor_scalar(out=y, in0=x, scalar1=s, scalar2=None, op0=ALU.mult)
-            if j >= PLAIN:
-                xf = groups.tile([P, GROUP], F32, name="xf%d" % i, tag="xf%d" % i)
-                live["xf", g, i] = xf
-                if g > 0:
-                    nc.scalar.copy(out=xf[:], in_=live["x", g, 1 - i][:, j, :])
-                else:
-                    nc.vector.tensor_copy(out=xf[:], in_=live["x", g, 1 - i][:, j, :])
+                nc.scalar.activation(out=y, in_=x, func=ACT.Copy, scale=s)
+                nc.vector.tensor_copy(out=xf, in_=xj)
 
-        def rest(g, piece):
-            i, j = divmod(piece, PACK)
-            if j == 0:
-                live["u", g, i] = groups.tile([P, PACK, GROUP], F32, name="u%d" % i, tag="u%d" % i)
-            nc.gpsimd.tensor_tensor(out=live["u", g, i][:, j, :], in0=live["x", g, 1 - i][:, j, :], in1=live["fe", g, i][:, j, :], op=ALU.add)
+        def rest(h):
+            block, i, g, cols = place(h)
+            live["u", h] = steps.tile([P, PACK, P], F32, name="u", tag="u", bufs=2)
+            nc.gpsimd.tensor_tensor(out=live["u", h][:], in0=live["x", g, 1 - i][:, :, cols], in1=live["fe", g, i][:, :, cols], op=ALU.add)
 
 
         def r_to_positions(h, q):
             block, i, g, cols = place(h)
             r = psum.tile([P, PACK * P], F32, name="r", tag="r", bufs=3)
             live["r", h] = r
-            y, xj = live["y", g, i], live["x", g, 1 - i]
-            nc.tensor.matmul(r[:, 3 * P : 4 * P], lhsT=live["xf", g, i][:, cols], rhs=ident_f[:], is_transpose=True, start=True, stop=False)
-            for j in (3, 2, 1, 0):
-                nc.tensor.matmul(r[:, j * P : j * P + P], lhsT=y[:, j, cols], rhs=ident_f[:], is_transpose=True, start=False, stop=False)
-            for j in (2, 1, 0):
-                nc.tensor.matmul(r[:, j * P : j * P + P], lhsT=xj[:, j, cols], rhs=ident_b[:], start=False, stop=(j == 0))
+            for kind in ("y", "xf"):
+                for j in range(PACK):
+                    nc.tensor.matmul(
+                        r[:, j * P : j * P + P], lhsT=live[kind, g, i][:, j, cols], rhs=ident_f[:], is_transpose=True,
+                        start=(kind == "y" and j == 0), stop=(kind == "xf" and j == PACK - 1),
+                    )
             if 0 <= q < GROUPS * TILES:
                 project(q, "acc", 2)
 
@@ -153,10 +150,17 @@ def tile_fr_pb_kernel(tc, x1, x2, FE_x1, FE_x2, g1, g2, p1_w, p1_b, p2_w, p2_b, 
             nc.scalar.activation(out=t[:], in_=live["xt", block][:, i, :], func=ACT.Copy, scale=live["s", block][:, i : i + 1])
 
         def xs_to_channels(h):
+            block, i, g, cols = place(h)
             z = psum.tile([P, PACK, P], F32, name="z", tag="z", bufs=2)
             live["z", h] = z
+            plain = by_matmul(h)
             for j in range(PACK):
-                nc.tensor.transpose(out=z[:, j, :], in_=live["xs", h][:, P * j : P * j + P], identity=ident_f[:])
+                nc.tensor.matmul(
+                    z[:, j, :], lhsT=live["xs", h][:, P * j : P * j + P], rhs=ident_f[:], is_transpose=True,
+                    start=(j == 0), stop=(j == PACK - 1 and not plain),
+                )
+            if plain:
+                nc.tensor.matmul(z[:], lhsT=ident_b[:], rhs=live["x", g, 1 - i][:, :, cols], start=False, stop=True)
 
         def fuse(h):
             block, i, g, cols = place(h)
@@ -165,7 +169,7 @@ def tile_fr_pb_kernel(tc, x1, x2, FE_x1, FE_x2, g1, g2, p1_w, p1_b, p2_w, p2_b, 
             nc.vector.tensor_tensor(
                 out=live["re", g][:, i, cols, :],
                 in0=live["z", h][:].rearrange("p j c -> p c j"),
-                in1=live["u", g, i][:, :, cols].rearrange("p j c -> p c j"),
+                in1=(live["fe", g, i][:, :, cols] if by_matmul(h) else live["u", h][:]).rearrange("p j c -> p c j"),
                 op=ALU.add,
             )
 
@@ -234,7 +238,8 @@ def tile_fr_pb_kernel(tc, x1, x2, FE_x1, FE_x2, g1, g2, p1_w, p1_b, p2_w, p2_b, 
             nc.vector.memset(t[:], 0.0)
             nc.sync.dma_start(out=t[0:n_rows, :], in_=src)
             rows.append(t)
-        load(0)
+        load("x", 0)
+        load("fe", 0)
         for name, src in (("b1r", p1_b), ("b2r", p2_b)):
             t = const.tile([P, PACK * P], BF16, name=name)
             nc.vector.memset(t[:], 0.0)
@@ -244,13 +249,14 @@ def tile_fr_pb_kernel(tc, x1, x2, FE_x1, FE_x2, g1, g2, p1_w, p1_b, p2_w, p2_b, 
         make_identity(nc, ident_b[:])
         ident_f = const.tile([P, P], F32, name="ident_f")
         make_identity(nc, ident_f[:])
-        load(1)
+        load("x", 1)
         w_raw = []
         for w in range(2):
             t = const.tile([P, 4, 1024], BF16, name="w_raw%d" % w)
             nc.sync.dma_start(out=t[:], in_=w_hbm[w])
             w_raw.append(t)
-        load(2)
+        load("fe", 1)
+        load("x", 2)
         w_codes = const.tile([P, 2 * TILES * P], U32, name="w_codes", align_bytes=64)
         w_scales = const.tile([P, 2 * TILES * P], U8, name="w_scales", align_bytes=64)
 
@@ -302,11 +308,12 @@ def tile_fr_pb_kernel(tc, x1, x2, FE_x1, FE_x2, g1, g2, p1_w, p1_b, p2_w, p2_b, 
                 else:
                     project(q, "acc", 2)
             if 0 <= q - 1 < GROUPS * TILES:
-                store(q - 1, q % 2 == 1 if late else q % 8 not in (1, 4, 7))
+                store(q - 1, q % 2 == 1 if late else q % 8 in (1, 4, 7))
             if phase == 5 and 1 <= g <= GROUPS:
                 quantise(g - 1)
-                hold = small.tile([P, 1], F32, name="hold", tag="hold")
-                nc.vector.tensor_copy(out=hold[:], in_=live["u", g - 1, 0][:, 0, 0:1])
+                if g + 2 < GROUPS:
+                    hold = small.tile([P, 1], F32, name="hold", tag="hold")
+                    nc.vector.tensor_copy(out=hold[:], in_=live["y", g, 0][:, 0, 0:1])
             if due(3) and (k - 3) % 2 == 0:
                 x_to_positions((k - 3) // 2)
             if 3 <= k < 3 + TILES:
@@ -320,7 +327,10 @@ def tile_fr_pb_kernel(tc, x1, x2, FE_x1, FE_x2, g1, g2, p1_w, p1_b, p2_w, p2_b, 
                     nc.vector.tensor_copy(out=bias[:, :, w : w + 1], in_=b_t[:, w, :, 0:1])
             if 0 <= (k + 9) // 8 < GROUPS:
                 gate((k + 9) // 8, (k + 9) % 8)
-            if 0 <= (k + 2) // 8 < GROUPS:
-                rest((k + 2) // 8, (k + 2) % 8)
-            if phase == 6 and 0 <= g and g + 3 < GROUPS:
-                load(g + 3)
+            if due(2) and not by_matmul(k - 2):
+                rest(k - 2)
+            if phase == 6 and 0 <= g:
+                if g + 3 < GROUPS:
+                    load("x", g + 3)
+                if g + 2 < GROUPS:
+                    load("fe", g + 2)

@@ -17,13 +17,22 @@ FLOPS = 2 * 1024 * 1024 * 4096
 P = 128
 PACK = 4
 GROUP = 512
+HALF = 256
 STEPS = 64
 GROUPS = 8
 TILES = 8
+OUTRIGHT = 3
+OUTRIGHT0 = 2
+FIRST_COPY = 2
+LATE = 2
 
 
 def by_matmul(h):
-    return h % 4 != 3
+    return h % 5 != 2
+
+
+def outright(g, j):
+    return j < (OUTRIGHT if g > 0 else OUTRIGHT0)
 
 
 def tile_fr_pb_kernel(tc, x1, x2, FE_x1, FE_x2, g1, g2, p1_w, p1_b, p2_w, p2_b, out_0, out_1):
@@ -58,20 +67,35 @@ def tile_fr_pb_kernel(tc, x1, x2, FE_x1, FE_x2, g1, g2, p1_w, p1_b, p2_w, p2_b, 
                 nc.sync.dma_start(out=t[:], in_=hbm[i][n][:, :, cols])
                 live[kind, g, i] = t
 
+        def gate_tiles(g, i):
+            live["y", g, i] = groups.tile([P, PACK, GROUP], F32, name="y%d" % i, tag="y%d" % i)
+            live["xf", g, i] = groups.tile([P, PACK - FIRST_COPY, GROUP], F32, name="xf%d" % i, tag="xf%d" % i)
+
+        def gate_first(half, i):
+            if half == 0:
+                gate_tiles(0, i)
+            c = slice(HALF * half, HALF * half + HALF)
+            for j in reversed(range(PACK)):
+                y, x, s = live["y", 0, i][:, j, c], live["x", 0, i][:, j, c], sig[:, j, 4 * i : 4 * i + 1]
+                xj = live["x", 0, 1 - i][:, j, c]
+                if outright(0, j):
+                    nc.vector.scalar_tensor_tensor(out=y, in0=x, scalar=s, in1=xj, op0=ALU.mult, op1=ALU.add)
+                else:
+                    nc.scalar.activation(out=y, in_=x, func=ACT.Copy, scale=s)
+                    nc.vector.tensor_copy(out=live["xf", 0, i][:, j - FIRST_COPY, c], in_=xj)
+
         def gate(g, piece):
             n = g // 2
             i, j = divmod(piece, PACK)
             if j == 0:
-                live["y", g, i] = groups.tile([P, PACK, GROUP], F32, name="y%d" % i, tag="y%d" % i)
-                live["xf", g, i] = groups.tile([P, PACK, GROUP], F32, name="xf%d" % i, tag="xf%d" % i)
+                gate_tiles(g, i)
             y, x, s = live["y", g, i][:, j, :], live["x", g, i][:, j, :], sig[:, j, 4 * i + n : 4 * i + n + 1]
-            xf, xj = live["xf", g, i][:, j, :], live["x", g, 1 - i][:, j, :]
-            if g > 0:
-                nc.gpsimd.tensor_scalar(out=y, in0=x, scalar1=s, scalar2=0.0, op0=ALU.mult, op1=ALU.add)
-                nc.gpsimd.tensor_scalar(out=xf, in0=xj, scalar1=1.0, scalar2=0.0, op0=ALU.mult, op1=ALU.add)
+            xj = live["x", g, 1 - i][:, j, :]
+            nc.gpsimd.tensor_scalar(out=y, in0=x, scalar1=s, scalar2=0.0, op0=ALU.mult, op1=ALU.add)
+            if outright(g, j):
+                nc.gpsimd.tensor_tensor(out=y, in0=y, in1=xj, op=ALU.add)
             else:
-                nc.scalar.activation(out=y, in_=x, func=ACT.Copy, scale=s)
-                nc.vector.tensor_copy(out=xf, in_=xj)
+                nc.gpsimd.tensor_scalar(out=live["xf", g, i][:, j - FIRST_COPY, :], in0=xj, scalar1=1.0, scalar2=0.0, op0=ALU.mult, op1=ALU.add)
 
         def rest(h):
             block, i, g, cols = place(h)
@@ -79,18 +103,14 @@ def tile_fr_pb_kernel(tc, x1, x2, FE_x1, FE_x2, g1, g2, p1_w, p1_b, p2_w, p2_b, 
             nc.gpsimd.tensor_tensor(out=live["u", h][:], in0=live["x", g, 1 - i][:, :, cols], in1=live["fe", g, i][:, :, cols], op=ALU.add)
 
 
-        def r_to_positions(h, q):
+        def r_to_positions(h):
             block, i, g, cols = place(h)
             r = psum.tile([P, PACK * P], F32, name="r", tag="r", bufs=3)
             live["r", h] = r
-            for kind in ("y", "xf"):
-                for j in range(PACK):
-                    nc.tensor.matmul(
-                        r[:, j * P : j * P + P], lhsT=live[kind, g, i][:, j, cols], rhs=ident_f[:], is_transpose=True,
-                        start=(kind == "y" and j == 0), stop=(kind == "xf" and j == PACK - 1),
-                    )
-            if 0 <= q < GROUPS * TILES:
-                project(q, "acc", 2)
+            parts = [(live["y", g, i][:, j, cols], j) for j in range(PACK)]
+            parts += [(live["xf", g, i][:, j - FIRST_COPY, cols], j) for j in range(PACK) if not outright(g, j)]
+            for at, (part, j) in enumerate(parts):
+                nc.tensor.matmul(r[:, j * P : j * P + P], lhsT=part, rhs=ident_f[:], is_transpose=True, start=(at == 0), stop=(at == len(parts) - 1))
 
         def exp_r(h):
             a = steps.tile([P, PACK * P], F32, name="a", tag="a")
@@ -166,45 +186,61 @@ def tile_fr_pb_kernel(tc, x1, x2, FE_x1, FE_x2, g1, g2, p1_w, p1_b, p2_w, p2_b, 
             block, i, g, cols = place(h)
             if h % 8 == 0:
                 live["re", g] = groups.tile([P, 2, GROUP, PACK], BF16, name="re", tag="re", align_bytes=64)
+            add = live["fe", g, i][:, :, cols] if by_matmul(h) else live["u", h][:]
             nc.vector.tensor_tensor(
-                out=live["re", g][:, i, cols, :],
-                in0=live["z", h][:].rearrange("p j c -> p c j"),
-                in1=(live["fe", g, i][:, :, cols] if by_matmul(h) else live["u", h][:]).rearrange("p j c -> p c j"),
+                out=live["re", g][:, i, cols, :].rearrange("p (c f) j -> p c j f", f=4),
+                in0=live["z", h][:].rearrange("p j (c f) -> p c j f", f=4),
+                in1=add.rearrange("p j (c f) -> p c j f", f=4),
                 op=ALU.add,
             )
 
 
-        def quantise(g):
-            codes = groups.tile([P, 2 * GROUP], U32, name="codes", tag="codes", align_bytes=64)
-            scales = groups.tile([P, 2 * GROUP], U8, name="scales", tag="scales", align_bytes=64)
-            live["codes", g] = codes
-            live["scales", g] = scales
-            nc.vector.quantize_mx(out=codes[:].bitcast(FP8X4), scales=scales[:], in_=live["re", g][:].rearrange("p i c j -> p (i c j)"))
+        def mx_tiles(g):
+            live["codes", g] = groups.tile([P, 2 * GROUP], U32, name="codes", tag="codes", align_bytes=64)
+            live["scales", g] = groups.tile([P, 2 * GROUP], U8, name="scales", tag="scales", align_bytes=64)
 
-        def project(q, tag, bufs):
-            g, m = divmod(q, TILES)
+        def quantise(g):
+            mx_tiles(g)
+            nc.vector.quantize_mx(
+                out=live["codes", g][:].bitcast(FP8X4), scales=live["scales", g][:], in_=live["re", g][:].rearrange("p i c j -> p (i c j)")
+            )
+
+        def quantise_half(g, half):
+            if half == 0:
+                mx_tiles(g)
+            for i in range(2):
+                c = slice(HALF * half, HALF * half + HALF)
+                w = slice(GROUP * i + HALF * half, GROUP * i + HALF * half + HALF)
+                nc.vector.quantize_mx(
+                    out=live["codes", g][:, w].bitcast(FP8X4), scales=live["scales", g][:, w],
+                    in_=live["re", g][:, i, c, :].rearrange("p c j -> p (c j)"),
+                )
+
+        def project(unit, tag, bufs):
+            g, m, first, width = unit
             acc = psum.tile([P, GROUP], F32, name="acc", tag=tag, bufs=bufs)
-            live["acc", q] = acc
+            live["acc", unit] = acc
             for i in range(2):
                 wc = slice((2 * m + i) * P, (2 * m + i) * P + P)
-                rc = slice(GROUP * i, GROUP * i + GROUP)
+                rc = slice(GROUP * i + first, GROUP * i + first + width)
                 nc.tensor.matmul_mx(
-                    out=acc[:], lhsT=w_codes[:, wc].bitcast(FP8X4), lhsT_scale=w_scales[:, wc],
+                    out=acc[:, 0:width], lhsT=w_codes[:, wc].bitcast(FP8X4), lhsT_scale=w_scales[:, wc],
                     rhs=live["codes", g][:, rc].bitcast(FP8X4), rhs_scale=live["scales", g][:, rc],
                     start=(i == 0), stop=(i == 1),
                 )
 
-        def store(q, on_vector):
-            g, m = divmod(q, TILES)
+        def store(unit, on_vector):
+            g, m, first, width = unit
             n, half = divmod(g, 2)
             w, mm = divmod(m, 4)
-            o = steps.tile([P, GROUP], F32, name="o", tag="o", bufs=6)
+            o = steps.tile([P, GROUP], F32, name="o", tag="o", bufs=12)
             b = bias[:, mm, w : w + 1]
+            acc = live["acc", unit][:, 0:width]
             if on_vector:
-                nc.vector.tensor_scalar(out=o[:], in0=live["acc", q][:], scalar1=b, scalar2=None, op0=ALU.add)
+                nc.vector.tensor_scalar(out=o[:, 0:width], in0=acc, scalar1=b, scalar2=None, op0=ALU.add)
             else:
-                nc.scalar.activation(out=o[:], in_=live["acc", q][:], func=ACT.Identity, bias=b, scale=1.0)
-            nc.sync.dma_start(out=out_hbm[w][n, mm][:, GROUP * half : GROUP * half + GROUP], in_=o[:])
+                nc.scalar.activation(out=o[:, 0:width], in_=acc, func=ACT.Identity, bias=b, scale=1.0)
+            nc.sync.dma_start(out=out_hbm[w][n, mm][:, GROUP * half + first : GROUP * half + first + width], in_=o[:, 0:width])
 
         def w_to_channels(m):
             w, mm = divmod(m, 4)
@@ -232,6 +268,9 @@ def tile_fr_pb_kernel(tc, x1, x2, FE_x1, FE_x2, g1, g2, p1_w, p1_b, p2_w, p2_b, 
                 )
 
 
+        warm = const.tile([P, 1], F32, name="warm")
+        nc.vector.memset(warm[:], 0.0)
+        nc.scalar.activation(out=warm[:], in_=warm[:], func=ACT.Exp)
         rows = []
         for name, src, n_rows in (("g1r", g1, 4), ("g2r", g2, 4)):
             t = const.tile([P, PACK * P], BF16, name=name)
@@ -239,6 +278,7 @@ def tile_fr_pb_kernel(tc, x1, x2, FE_x1, FE_x2, g1, g2, p1_w, p1_b, p2_w, p2_b, 
             nc.sync.dma_start(out=t[0:n_rows, :], in_=src)
             rows.append(t)
         load("x", 0)
+        load("x", 1)
         load("fe", 0)
         for name, src in (("b1r", p1_b), ("b2r", p2_b)):
             t = const.tile([P, PACK * P], BF16, name=name)
@@ -249,7 +289,6 @@ def tile_fr_pb_kernel(tc, x1, x2, FE_x1, FE_x2, g1, g2, p1_w, p1_b, p2_w, p2_b, 
         make_identity(nc, ident_b[:])
         ident_f = const.tile([P, P], F32, name="ident_f")
         make_identity(nc, ident_f[:])
-        load("x", 1)
         w_raw = []
         for w in range(2):
             t = const.tile([P, 4, 1024], BF16, name="w_raw%d" % w)
@@ -273,13 +312,17 @@ def tile_fr_pb_kernel(tc, x1, x2, FE_x1, FE_x2, g1, g2, p1_w, p1_b, p2_w, p2_b, 
         nc.vector.reciprocal(out=sig[:], in_=sig[:])
         bias = const.tile([P, 4, 2], F32, name="bias")
 
-
+        waiting = []
+        projected = []
+        count = 0
         for k in range(-9, STEPS + 15):
             g, phase = divmod(k, 8)
 
             def due(lag):
                 return 0 <= k - lag < STEPS
 
+            if k in (-2, -1):
+                gate_first(0, k + 2)
             if due(0):
                 exp_r(k)
             if due(1):
@@ -298,22 +341,31 @@ def tile_fr_pb_kernel(tc, x1, x2, FE_x1, FE_x2, g1, g2, p1_w, p1_b, p2_w, p2_b, 
                 w_quantise(k - 4)
             if due(5):
                 xs_to_channels(k - 5)
-            q = k - 14
-            late = k >= STEPS
             if due(-1):
-                r_to_positions(k + 1, q)
-            elif 0 <= q < GROUPS * TILES:
-                if late and q % 2 == 1:
-                    project(q, "r", 3)
+                r_to_positions(k + 1)
+            late = k >= STEPS
+            old = projected
+            projected = []
+            for unit in waiting[: LATE if late else 1]:
+                if k > STEPS and count % 2 == 1:
+                    project(unit, "r", 3)
                 else:
-                    project(q, "acc", 2)
-            if 0 <= q - 1 < GROUPS * TILES:
-                store(q - 1, q % 2 == 1 if late else q % 8 in (1, 4, 7))
-            if phase == 5 and 1 <= g <= GROUPS:
+                    project(unit, "acc", 2)
+                count += 1
+                projected.append(unit)
+            waiting = waiting[len(projected) :]
+            for at, unit in enumerate(old):
+                store(unit, at % 2 == 1 if late else unit[1] in (1, 4, 7))
+            if phase == 5 and 1 <= g < GROUPS:
                 quantise(g - 1)
+                waiting += [(g - 1, m, 0, GROUP) for m in range(TILES)]
                 if g + 2 < GROUPS:
                     hold = small.tile([P, 1], F32, name="hold", tag="hold")
                     nc.vector.tensor_copy(out=hold[:], in_=live["y", g, 0][:, 0, 0:1])
+            if k in (STEPS + 1, STEPS + 5):
+                half = (k - STEPS) // 4
+                quantise_half(GROUPS - 1, half)
+                waiting += [(GROUPS - 1, m, HALF * half, HALF) for m in range(TILES)]
             if due(3) and (k - 3) % 2 == 0:
                 x_to_positions((k - 3) // 2)
             if 3 <= k < 3 + TILES:
@@ -325,7 +377,9 @@ def tile_fr_pb_kernel(tc, x1, x2, FE_x1, FE_x2, g1, g2, p1_w, p1_b, p2_w, p2_b, 
                         nc.tensor.transpose(out=b_t[:, w, mm, :], in_=rows[2 + w][:, P * mm : P * mm + P], identity=ident_b[:])
                 for w in range(2):
                     nc.vector.tensor_copy(out=bias[:, :, w : w + 1], in_=b_t[:, w, :, 0:1])
-            if 0 <= (k + 9) // 8 < GROUPS:
+            if k in (-1, 0):
+                gate_first(1, k + 1)
+            if 1 <= (k + 9) // 8 < GROUPS:
                 gate((k + 9) // 8, (k + 9) % 8)
             if due(2) and not by_matmul(k - 2):
                 rest(k - 2)

@@ -91,11 +91,18 @@ def tile_fr_pb_kernel(tc, x1, x2, FE_x1, FE_x2, g1, g2, p1_w, p1_b, p2_w, p2_b, 
                 gate_tiles(g, i)
             y, x, s = live["y", g, i][:, j, :], live["x", g, i][:, j, :], sig[:, j, 4 * i + n : 4 * i + n + 1]
             xj = live["x", g, 1 - i][:, j, :]
-            nc.gpsimd.tensor_scalar(out=y, in0=x, scalar1=s, scalar2=0.0, op0=ALU.mult, op1=ALU.add)
+            if j == 3:
+                nc.scalar.activation(out=y, in_=x, func=ACT.Copy, scale=s)
+            else:
+                nc.gpsimd.tensor_scalar(out=y, in0=x, scalar1=s, scalar2=0.0, op0=ALU.mult, op1=ALU.add)
+            if adds:
+                nc.gpsimd.tensor_tensor(**adds.pop())
             if outright(g, j):
-                nc.gpsimd.tensor_tensor(out=y, in0=y, in1=xj, op=ALU.add)
+                adds.append(dict(out=y, in0=y, in1=xj, op=ALU.add))
             else:
                 nc.gpsimd.tensor_scalar(out=live["xf", g, i][:, j - FIRST_COPY, :], in0=xj, scalar1=1.0, scalar2=0.0, op0=ALU.mult, op1=ALU.add)
+
+        adds = []
 
         def rest(h):
             block, i, g, cols = place(h)
@@ -346,7 +353,7 @@ def tile_fr_pb_kernel(tc, x1, x2, FE_x1, FE_x2, g1, g2, p1_w, p1_b, p2_w, p2_b, 
             late = k >= STEPS
             old = projected
             projected = []
-            for unit in waiting[: LATE if late else 1]:
+            for unit in waiting[: LATE if late or k % 2 == 0 else 0]:
                 if k > STEPS and count % 2 == 1:
                     project(unit, "r", 3)
                 else:
@@ -355,7 +362,7 @@ def tile_fr_pb_kernel(tc, x1, x2, FE_x1, FE_x2, g1, g2, p1_w, p1_b, p2_w, p2_b, 
                 projected.append(unit)
             waiting = waiting[len(projected) :]
             for at, unit in enumerate(old):
-                store(unit, at % 2 == 1 if late else unit[1] in (1, 4, 7))
+                store(unit, at % 2 == 1)
             if phase == 5 and 1 <= g < GROUPS:
                 quantise(g - 1)
                 waiting += [(g - 1, m, 0, GROUP) for m in range(TILES)]

@@ -22,7 +22,7 @@ STEPS = 64
 GROUPS = 8
 TILES = 8
 OUTRIGHT = 3
-OUTRIGHT0 = 2
+OUTRIGHT0 = 4
 FIRST_COPY = 2
 LATE = 2
 
@@ -91,10 +91,7 @@ def tile_fr_pb_kernel(tc, x1, x2, FE_x1, FE_x2, g1, g2, p1_w, p1_b, p2_w, p2_b, 
                 gate_tiles(g, i)
             y, x, s = live["y", g, i][:, j, :], live["x", g, i][:, j, :], sig[:, j, 4 * i + n : 4 * i + n + 1]
             xj = live["x", g, 1 - i][:, j, :]
-            if j == 3:
-                nc.scalar.activation(out=y, in_=x, func=ACT.Copy, scale=s)
-            else:
-                nc.gpsimd.tensor_scalar(out=y, in0=x, scalar1=s, scalar2=0.0, op0=ALU.mult, op1=ALU.add)
+            nc.gpsimd.tensor_scalar(out=y, in0=x, scalar1=s, scalar2=0.0, op0=ALU.mult, op1=ALU.add)
             if adds:
                 nc.gpsimd.tensor_tensor(**adds.pop())
             if outright(g, j):
@@ -285,7 +282,13 @@ def tile_fr_pb_kernel(tc, x1, x2, FE_x1, FE_x2, g1, g2, p1_w, p1_b, p2_w, p2_b, 
             nc.sync.dma_start(out=t[0:n_rows, :], in_=src)
             rows.append(t)
         load("x", 0)
-        load("x", 1)
+        w_raw = []
+        for w in range(2):
+            t = const.tile([P, 4, 1024], BF16, name="w_raw%d" % w)
+            nc.sync.dma_start(out=t[:], in_=w_hbm[w])
+            w_raw.append(t)
+            if w == 0:
+                load("x", 1)
         load("fe", 0)
         for name, src in (("b1r", p1_b), ("b2r", p2_b)):
             t = const.tile([P, PACK * P], BF16, name=name)
@@ -296,11 +299,6 @@ def tile_fr_pb_kernel(tc, x1, x2, FE_x1, FE_x2, g1, g2, p1_w, p1_b, p2_w, p2_b, 
         make_identity(nc, ident_b[:])
         ident_f = const.tile([P, P], F32, name="ident_f")
         make_identity(nc, ident_f[:])
-        w_raw = []
-        for w in range(2):
-            t = const.tile([P, 4, 1024], BF16, name="w_raw%d" % w)
-            nc.sync.dma_start(out=t[:], in_=w_hbm[w])
-            w_raw.append(t)
         load("fe", 1)
         load("x", 2)
         w_codes = const.tile([P, 2 * TILES * P], U32, name="w_codes", align_bytes=64)
@@ -344,8 +342,9 @@ def tile_fr_pb_kernel(tc, x1, x2, FE_x1, FE_x2, g1, g2, p1_w, p1_b, p2_w, p2_b, 
                 divide(k - 3)
             if due(4):
                 scale_x(k - 4)
-            if 4 <= k < 4 + TILES:
-                w_quantise(k - 4)
+            if 1 <= k < 1 + TILES // 2:
+                for m in (2 * k - 2, 2 * k - 1):
+                    w_quantise(m)
             if due(5):
                 xs_to_channels(k - 5)
             if due(-1):
@@ -353,7 +352,7 @@ def tile_fr_pb_kernel(tc, x1, x2, FE_x1, FE_x2, g1, g2, p1_w, p1_b, p2_w, p2_b, 
             late = k >= STEPS
             old = projected
             projected = []
-            for unit in waiting[: LATE if late or k % 2 == 0 else 0]:
+            for unit in waiting[: LATE if late else 1]:
                 if k > STEPS and count % 2 == 1:
                     project(unit, "r", 3)
                 else:
@@ -362,7 +361,7 @@ def tile_fr_pb_kernel(tc, x1, x2, FE_x1, FE_x2, g1, g2, p1_w, p1_b, p2_w, p2_b, 
                 projected.append(unit)
             waiting = waiting[len(projected) :]
             for at, unit in enumerate(old):
-                store(unit, at % 2 == 1)
+                store(unit, at % 2 == 1 if late else unit[1] in (1, 4, 7))
             if phase == 5 and 1 <= g < GROUPS:
                 quantise(g - 1)
                 waiting += [(g - 1, m, 0, GROUP) for m in range(TILES)]
@@ -375,9 +374,10 @@ def tile_fr_pb_kernel(tc, x1, x2, FE_x1, FE_x2, g1, g2, p1_w, p1_b, p2_w, p2_b, 
                 waiting += [(GROUPS - 1, m, HALF * half, HALF) for m in range(TILES)]
             if due(3) and (k - 3) % 2 == 0:
                 x_to_positions((k - 3) // 2)
-            if 3 <= k < 3 + TILES:
-                w_to_channels(k - 3)
-            if k == 2:
+            if 0 <= k < TILES // 2:
+                for m in (2 * k, 2 * k + 1):
+                    w_to_channels(m)
+            if k == 8:
                 b_t = psum.tile([P, 2, 4, P], BF16, name="b_t", tag="acc", bufs=2)
                 for w in range(2):
                     for mm in range(4):

@@ -21,9 +21,7 @@ HALF = 256
 STEPS = 64
 GROUPS = 8
 TILES = 8
-OUTRIGHT = 3
-OUTRIGHT0 = 4
-FIRST_COPY = 2
+OUTRIGHT = 2
 LATE = 2
 
 
@@ -32,7 +30,7 @@ def by_matmul(h):
 
 
 def outright(g, j):
-    return j < (OUTRIGHT if g > 0 else OUTRIGHT0)
+    return g == 0 or j < OUTRIGHT
 
 
 def tile_fr_pb_kernel(tc, x1, x2, FE_x1, FE_x2, g1, g2, p1_w, p1_b, p2_w, p2_b, out_0, out_1):
@@ -69,7 +67,8 @@ def tile_fr_pb_kernel(tc, x1, x2, FE_x1, FE_x2, g1, g2, p1_w, p1_b, p2_w, p2_b, 
 
         def gate_tiles(g, i):
             live["y", g, i] = groups.tile([P, PACK, GROUP], F32, name="y%d" % i, tag="y%d" % i)
-            live["xf", g, i] = groups.tile([P, PACK - FIRST_COPY, GROUP], F32, name="xf%d" % i, tag="xf%d" % i)
+            if g > 0 and OUTRIGHT < PACK:
+                live["xf", g, i] = groups.tile([P, PACK - OUTRIGHT, GROUP], F32, name="xf%d" % i, tag="xf%d" % i)
 
         def gate_first(half, i):
             if half == 0:
@@ -78,11 +77,7 @@ def tile_fr_pb_kernel(tc, x1, x2, FE_x1, FE_x2, g1, g2, p1_w, p1_b, p2_w, p2_b, 
             for j in reversed(range(PACK)):
                 y, x, s = live["y", 0, i][:, j, c], live["x", 0, i][:, j, c], sig[:, j, 4 * i : 4 * i + 1]
                 xj = live["x", 0, 1 - i][:, j, c]
-                if outright(0, j):
-                    nc.vector.scalar_tensor_tensor(out=y, in0=x, scalar=s, in1=xj, op0=ALU.mult, op1=ALU.add)
-                else:
-                    nc.scalar.activation(out=y, in_=x, func=ACT.Copy, scale=s)
-                    nc.vector.tensor_copy(out=live["xf", 0, i][:, j - FIRST_COPY, c], in_=xj)
+                nc.vector.scalar_tensor_tensor(out=y, in0=x, scalar=s, in1=xj, op0=ALU.mult, op1=ALU.add)
 
         def gate(g, piece):
             n = g // 2
@@ -90,16 +85,15 @@ def tile_fr_pb_kernel(tc, x1, x2, FE_x1, FE_x2, g1, g2, p1_w, p1_b, p2_w, p2_b, 
             if j == 0:
                 gate_tiles(g, i)
             y, x, s = live["y", g, i][:, j, :], live["x", g, i][:, j, :], sig[:, j, 4 * i + n : 4 * i + n + 1]
-            xj = live["x", g, 1 - i][:, j, :]
+            xj = live["x", g, 1 - i]
             nc.gpsimd.tensor_scalar(out=y, in0=x, scalar1=s, scalar2=0.0, op0=ALU.mult, op1=ALU.add)
-            if adds:
-                nc.gpsimd.tensor_tensor(**adds.pop())
-            if outright(g, j):
-                adds.append(dict(out=y, in0=y, in1=xj, op=ALU.add))
-            else:
-                nc.gpsimd.tensor_scalar(out=live["xf", g, i][:, j - FIRST_COPY, :], in0=xj, scalar1=1.0, scalar2=0.0, op0=ALU.mult, op1=ALU.add)
-
-        adds = []
+            if j == OUTRIGHT - 1:
+                xo, yo = xj[:, 0:OUTRIGHT, :], live["y", g, i][:, 0:OUTRIGHT, :]
+                nc.gpsimd.tensor_tensor(out=yo, in0=yo, in1=xo, op=ALU.add)
+            if j == PACK - 1 and OUTRIGHT < PACK:
+                nc.gpsimd.tensor_scalar(
+                    out=live["xf", g, i][:], in0=xj[:, OUTRIGHT:PACK, :], scalar1=1.0, scalar2=0.0, op0=ALU.mult, op1=ALU.add
+                )
 
         def rest(h):
             block, i, g, cols = place(h)
@@ -112,7 +106,7 @@ def tile_fr_pb_kernel(tc, x1, x2, FE_x1, FE_x2, g1, g2, p1_w, p1_b, p2_w, p2_b, 
             r = psum.tile([P, PACK * P], F32, name="r", tag="r", bufs=3)
             live["r", h] = r
             parts = [(live["y", g, i][:, j, cols], j) for j in range(PACK)]
-            parts += [(live["xf", g, i][:, j - FIRST_COPY, cols], j) for j in range(PACK) if not outright(g, j)]
+            parts += [(live["xf", g, i][:, j - OUTRIGHT, cols], j) for j in range(PACK) if not outright(g, j)]
             for at, (part, j) in enumerate(parts):
                 nc.tensor.matmul(r[:, j * P : j * P + P], lhsT=part, rhs=ident_f[:], is_transpose=True, start=(at == 0), stop=(at == len(parts) - 1))
 
@@ -282,13 +276,12 @@ def tile_fr_pb_kernel(tc, x1, x2, FE_x1, FE_x2, g1, g2, p1_w, p1_b, p2_w, p2_b, 
             nc.sync.dma_start(out=t[0:n_rows, :], in_=src)
             rows.append(t)
         load("x", 0)
+        load("x", 1)
         w_raw = []
         for w in range(2):
             t = const.tile([P, 4, 1024], BF16, name="w_raw%d" % w)
             nc.sync.dma_start(out=t[:], in_=w_hbm[w])
             w_raw.append(t)
-            if w == 0:
-                load("x", 1)
         load("fe", 0)
         for name, src in (("b1r", p1_b), ("b2r", p2_b)):
             t = const.tile([P, PACK * P], BF16, name=name)

@@ -21,12 +21,13 @@ HALF = 256
 STEPS = 64
 GROUPS = 8
 TILES = 8
+XF_AT = 3
 OUTRIGHT = 2
 LATE = 2
 
 
 def by_matmul(h):
-    return h % 5 != 2
+    return h // 2 % 5 != 1
 
 
 def outright(g, j):
@@ -60,53 +61,53 @@ def tile_fr_pb_kernel(tc, x1, x2, FE_x1, FE_x2, g1, g2, p1_w, p1_b, p2_w, p2_b, 
             n, half = divmod(g, 2)
             cols = slice(GROUP * half, GROUP * half + GROUP)
             hbm, bufs = {"x": (x_hbm, 4), "fe": (fe_hbm, 3)}[kind]
+            t = groups.tile([P, 2, PACK, GROUP], BF16, name=kind, tag=kind, bufs=bufs)
+            live[kind, g] = t
             for i in range(2):
-                t = groups.tile([P, PACK, GROUP], BF16, name="%s%d" % (kind, i), tag="%s%d" % (kind, i), bufs=bufs)
-                nc.sync.dma_start(out=t[:], in_=hbm[i][n][:, :, cols])
-                live[kind, g, i] = t
+                nc.sync.dma_start(out=t[:, i if kind == "x" else 1 - i], in_=hbm[i][n][:, :, cols])
 
-        def gate_tiles(g, i):
-            live["y", g, i] = groups.tile([P, PACK, GROUP], F32, name="y%d" % i, tag="y%d" % i)
-            if g > 0 and OUTRIGHT < PACK:
-                live["xf", g, i] = groups.tile([P, PACK - OUTRIGHT, GROUP], F32, name="xf%d" % i, tag="xf%d" % i)
+        def gate_tiles(g):
+            live["y", g] = groups.tile([P, 2, PACK, GROUP], F32, name="y", tag="y")
+            if g > 0:
+                live["xf", g] = groups.tile([P, 2, PACK - OUTRIGHT, GROUP], F32, name="xf", tag="xf")
 
         def gate_first(half, i):
-            if half == 0:
-                gate_tiles(0, i)
+            if half == 0 and i == 0:
+                gate_tiles(0)
             c = slice(HALF * half, HALF * half + HALF)
             for j in reversed(range(PACK)):
-                y, x, s = live["y", 0, i][:, j, c], live["x", 0, i][:, j, c], sig[:, j, 4 * i : 4 * i + 1]
-                xj = live["x", 0, 1 - i][:, j, c]
+                y, x, s = live["y", 0][:, 1 - i, j, c], live["x", 0][:, i, j, c], sig[:, j, 4 * i : 4 * i + 1]
+                xj = live["x", 0][:, 1 - i, j, c]
                 nc.vector.scalar_tensor_tensor(out=y, in0=x, scalar=s, in1=xj, op0=ALU.mult, op1=ALU.add)
 
         def gate(g, piece):
             n = g // 2
             i, j = divmod(piece, PACK)
-            if j == 0:
-                gate_tiles(g, i)
-            y, x, s = live["y", g, i][:, j, :], live["x", g, i][:, j, :], sig[:, j, 4 * i + n : 4 * i + n + 1]
-            xj = live["x", g, 1 - i]
+            if piece == 0:
+                gate_tiles(g)
+            y, x, s = live["y", g][:, 1 - i, j, :], live["x", g][:, i, j, :], sig[:, j, 4 * i + n : 4 * i + n + 1]
             nc.gpsimd.tensor_scalar(out=y, in0=x, scalar1=s, scalar2=0.0, op0=ALU.mult, op1=ALU.add)
-            if j == OUTRIGHT - 1:
-                xo, yo = xj[:, 0:OUTRIGHT, :], live["y", g, i][:, 0:OUTRIGHT, :]
-                nc.gpsimd.tensor_tensor(out=yo, in0=yo, in1=xo, op=ALU.add)
-            if j == PACK - 1 and OUTRIGHT < PACK:
+            if piece == XF_AT:
                 nc.gpsimd.tensor_scalar(
-                    out=live["xf", g, i][:], in0=xj[:, OUTRIGHT:PACK, :], scalar1=1.0, scalar2=0.0, op0=ALU.mult, op1=ALU.add
+                    out=live["xf", g][:], in0=live["x", g][:, :, OUTRIGHT:PACK, :], scalar1=1.0, scalar2=0.0, op0=ALU.mult, op1=ALU.add
                 )
+            if piece == 2 * PACK - 1:
+                yo = live["y", g][:, :, 0:OUTRIGHT, :]
+                nc.gpsimd.tensor_tensor(out=yo, in0=yo, in1=live["x", g][:, :, 0:OUTRIGHT, :], op=ALU.add)
 
-        def rest(h):
-            block, i, g, cols = place(h)
-            live["u", h] = steps.tile([P, PACK, P], F32, name="u", tag="u", bufs=2)
-            nc.gpsimd.tensor_tensor(out=live["u", h][:], in0=live["x", g, 1 - i][:, :, cols], in1=live["fe", g, i][:, :, cols], op=ALU.add)
+        def rest(block):
+            g, b = divmod(block, 4)
+            cols = slice(P * b, P * b + P)
+            live["u", block] = steps.tile([P, 2, PACK, P], F32, name="u", tag="u", bufs=2)
+            nc.gpsimd.tensor_tensor(out=live["u", block][:], in0=live["x", g][:, :, :, cols], in1=live["fe", g][:, :, :, cols], op=ALU.add)
 
 
         def r_to_positions(h):
             block, i, g, cols = place(h)
             r = psum.tile([P, PACK * P], F32, name="r", tag="r", bufs=3)
             live["r", h] = r
-            parts = [(live["y", g, i][:, j, cols], j) for j in range(PACK)]
-            parts += [(live["xf", g, i][:, j - OUTRIGHT, cols], j) for j in range(PACK) if not outright(g, j)]
+            parts = [(live["y", g][:, 1 - i, j, cols], j) for j in range(PACK)]
+            parts += [(live["xf", g][:, 1 - i, j - OUTRIGHT, cols], j) for j in range(PACK) if not outright(g, j)]
             for at, (part, j) in enumerate(parts):
                 nc.tensor.matmul(r[:, j * P : j * P + P], lhsT=part, rhs=ident_f[:], is_transpose=True, start=(at == 0), stop=(at == len(parts) - 1))
 
@@ -159,7 +160,7 @@ def tile_fr_pb_kernel(tc, x1, x2, FE_x1, FE_x2, g1, g2, p1_w, p1_b, p2_w, p2_b, 
             live["xt", block] = xt
             for i in range(2):
                 for j in range(PACK):
-                    nc.tensor.transpose(out=xt[:, i, P * j : P * j + P], in_=live["x", g, i][:, j, cols], identity=ident_b[:])
+                    nc.tensor.transpose(out=xt[:, i, P * j : P * j + P], in_=live["x", g][:, i, j, cols], identity=ident_b[:])
 
         def scale_x(h):
             block, i, g, cols = place(h)
@@ -178,13 +179,13 @@ def tile_fr_pb_kernel(tc, x1, x2, FE_x1, FE_x2, g1, g2, p1_w, p1_b, p2_w, p2_b, 
                     start=(j == 0), stop=(j == PACK - 1 and not plain),
                 )
             if plain:
-                nc.tensor.matmul(z[:], lhsT=ident_b[:], rhs=live["x", g, 1 - i][:, :, cols], start=False, stop=True)
+                nc.tensor.matmul(z[:], lhsT=ident_b[:], rhs=live["x", g][:, 1 - i, :, cols], start=False, stop=True)
 
         def fuse(h):
             block, i, g, cols = place(h)
             if h % 8 == 0:
                 live["re", g] = groups.tile([P, 2, GROUP, PACK], BF16, name="re", tag="re", align_bytes=64)
-            add = live["fe", g, i][:, :, cols] if by_matmul(h) else live["u", h][:]
+            add = live["fe", g][:, 1 - i, :, cols] if by_matmul(h) else live["u", block][:, 1 - i]
             nc.vector.tensor_tensor(
                 out=live["re", g][:, i, cols, :].rearrange("p (c f) j -> p c j f", f=4),
                 in0=live["z", h][:].rearrange("p j (c f) -> p c j f", f=4),
@@ -354,13 +355,13 @@ def tile_fr_pb_kernel(tc, x1, x2, FE_x1, FE_x2, g1, g2, p1_w, p1_b, p2_w, p2_b, 
                 projected.append(unit)
             waiting = waiting[len(projected) :]
             for at, unit in enumerate(old):
-                store(unit, at % 2 == 1 if late else unit[1] in (1, 4, 7))
+                store(unit, at % 2 == 1 if late else unit[1] in (0, 2, 4))
             if phase == 5 and 1 <= g < GROUPS:
                 quantise(g - 1)
                 waiting += [(g - 1, m, 0, GROUP) for m in range(TILES)]
                 if g + 2 < GROUPS:
                     hold = small.tile([P, 1], F32, name="hold", tag="hold")
-                    nc.vector.tensor_copy(out=hold[:], in_=live["y", g, 0][:, 0, 0:1])
+                    nc.vector.tensor_copy(out=hold[:], in_=live["y", g][:, 1, 0, 0:1])
             if k in (STEPS + 1, STEPS + 5):
                 half = (k - STEPS) // 4
                 quantise_half(GROUPS - 1, half)
@@ -381,8 +382,8 @@ def tile_fr_pb_kernel(tc, x1, x2, FE_x1, FE_x2, g1, g2, p1_w, p1_b, p2_w, p2_b, 
                 gate_first(1, k + 1)
             if 1 <= (k + 9) // 8 < GROUPS:
                 gate((k + 9) // 8, (k + 9) % 8)
-            if due(2) and not by_matmul(k - 2):
-                rest(k - 2)
+            if due(0) and k % 2 == 0 and not by_matmul(k):
+                rest(k // 2)
             if phase == 6 and 0 <= g:
                 if g + 3 < GROUPS:
                     load("x", g + 3)

@@ -23,11 +23,10 @@ GROUPS = 8
 TILES = 8
 XF_AT = 3
 OUTRIGHT = 2
-LATE = 2
 
 
 def by_matmul(h):
-    return h // 2 % 5 != 1
+    return h < 8 or h % 8 >= 2
 
 
 def outright(g, j):
@@ -91,9 +90,10 @@ def tile_fr_pb_kernel(tc, x1, x2, FE_x1, FE_x2, g1, g2, p1_w, p1_b, p2_w, p2_b, 
                 nc.gpsimd.tensor_scalar(
                     out=live["xf", g][:], in0=live["x", g][:, :, OUTRIGHT:PACK, :], scalar1=1.0, scalar2=0.0, op0=ALU.mult, op1=ALU.add
                 )
-            if piece == 2 * PACK - 1:
-                yo = live["y", g][:, :, 0:OUTRIGHT, :]
-                nc.gpsimd.tensor_tensor(out=yo, in0=yo, in1=live["x", g][:, :, 0:OUTRIGHT, :], op=ALU.add)
+            if j == PACK - 1 and (g == 1 or i == 1):
+                o = slice(1 - i, 2 - i) if g == 1 else slice(0, 2)
+                yo = live["y", g][:, o, 0:OUTRIGHT, :]
+                nc.gpsimd.tensor_tensor(out=yo, in0=yo, in1=live["x", g][:, o, 0:OUTRIGHT, :], op=ALU.add)
 
         def rest(block):
             g, b = divmod(block, 4)
@@ -153,10 +153,10 @@ def tile_fr_pb_kernel(tc, x1, x2, FE_x1, FE_x2, g1, g2, p1_w, p1_b, p2_w, p2_b, 
             )
 
 
-        def x_to_positions(block):
+        def x_to_positions(block, tag="xt", bufs=1):
             g, b = divmod(block, 4)
             cols = slice(P * b, P * b + P)
-            xt = psum.tile([P, 2, PACK * P], BF16, name="xt", tag="xt", bufs=1)
+            xt = psum.tile([P, 2, PACK * P], BF16, name="xt", tag=tag, bufs=bufs)
             live["xt", block] = xt
             for i in range(2):
                 for j in range(PACK):
@@ -164,7 +164,7 @@ def tile_fr_pb_kernel(tc, x1, x2, FE_x1, FE_x2, g1, g2, p1_w, p1_b, p2_w, p2_b, 
 
         def scale_x(h):
             block, i, g, cols = place(h)
-            t = steps.tile([P, PACK * P], F32, name="xs", tag="xs")
+            t = steps.tile([P, PACK * P], F32, name="xs", tag="xs", bufs=4)
             live["xs", h] = t
             nc.scalar.activation(out=t[:], in_=live["xt", block][:, i, :], func=ACT.Copy, scale=live["s", block][:, i : i + 1])
 
@@ -267,15 +267,13 @@ def tile_fr_pb_kernel(tc, x1, x2, FE_x1, FE_x2, g1, g2, p1_w, p1_b, p2_w, p2_b, 
                 )
 
 
+        g_rows = const.tile([P, PACK * P], BF16, name="g_rows")
+        nc.vector.memset(g_rows[:], 0.0)
+        for i, src in enumerate((g1, g2)):
+            nc.sync.dma_start(out=g_rows[4 * i : 4 * i + 4, :], in_=src)
         warm = const.tile([P, 1], F32, name="warm")
         nc.vector.memset(warm[:], 0.0)
         nc.scalar.activation(out=warm[:], in_=warm[:], func=ACT.Exp)
-        rows = []
-        for name, src, n_rows in (("g1r", g1, 4), ("g2r", g2, 4)):
-            t = const.tile([P, PACK * P], BF16, name=name)
-            nc.vector.memset(t[:], 0.0)
-            nc.sync.dma_start(out=t[0:n_rows, :], in_=src)
-            rows.append(t)
         load("x", 0)
         load("x", 1)
         w_raw = []
@@ -284,11 +282,10 @@ def tile_fr_pb_kernel(tc, x1, x2, FE_x1, FE_x2, g1, g2, p1_w, p1_b, p2_w, p2_b, 
             nc.sync.dma_start(out=t[:], in_=w_hbm[w])
             w_raw.append(t)
         load("fe", 0)
-        for name, src in (("b1r", p1_b), ("b2r", p2_b)):
-            t = const.tile([P, PACK * P], BF16, name=name)
-            nc.vector.memset(t[:], 0.0)
-            nc.sync.dma_start(out=t[0:1, :], in_=src.rearrange("(o c) -> o c", o=1))
-            rows.append(t)
+        b_rows = const.tile([P, PACK * P], BF16, name="b_rows")
+        nc.vector.memset(b_rows[:], 0.0)
+        for w, src in enumerate((p1_b, p2_b)):
+            nc.sync.dma_start(out=b_rows[w : w + 1, :], in_=src.rearrange("(o c) -> o c", o=1))
         ident_b = const.tile([P, P], BF16, name="ident_b")
         make_identity(nc, ident_b[:])
         ident_f = const.tile([P, P], F32, name="ident_f")
@@ -298,23 +295,20 @@ def tile_fr_pb_kernel(tc, x1, x2, FE_x1, FE_x2, g1, g2, p1_w, p1_b, p2_w, p2_b, 
         w_codes = const.tile([P, 2 * TILES * P], U32, name="w_codes", align_bytes=64)
         w_scales = const.tile([P, 2 * TILES * P], U8, name="w_scales", align_bytes=64)
 
-        g_t = psum.tile([P, 2, PACK, P], BF16, name="g_t", tag="xt", bufs=1)
-        for i in range(2):
-            by_j = const.tile([P, PACK, P], BF16, name="by_j%d" % i)
-            nc.vector.tensor_copy(out=by_j[:], in_=rows[i][:].rearrange("r (p j) -> r j p", j=PACK))
-            for j in range(PACK):
-                nc.tensor.transpose(out=g_t[:, i, j, :], in_=by_j[:, j, :], identity=ident_b[:])
+        g_t = psum.tile([P, PACK, P], BF16, name="g_t", tag="xt", bufs=1)
+        by_j = const.tile([P, PACK, P], BF16, name="by_j")
+        nc.vector.tensor_copy(out=by_j[:], in_=g_rows[:].rearrange("r (p j) -> r j p", j=PACK))
+        for j in range(PACK):
+            nc.tensor.transpose(out=g_t[:, j, :], in_=by_j[:, j, :], identity=ident_b[:])
         sig = const.tile([P, PACK, 8], F32, name="sig")
-        for i in range(2):
-            nc.scalar.activation(out=sig[:, :, 4 * i : 4 * i + 4], in_=g_t[:, i, :, 0:4], func=ACT.Exp, scale=-1.0)
+        nc.scalar.activation(out=sig[:], in_=g_t[:, :, 0:8], func=ACT.Exp, scale=-1.0)
         nc.vector.tensor_scalar(out=sig[:], in0=sig[:], scalar1=1.0, scalar2=None, op0=ALU.add)
         nc.vector.reciprocal(out=sig[:], in_=sig[:])
         bias = const.tile([P, 4, 2], F32, name="bias")
 
         waiting = []
         projected = []
-        count = 0
-        for k in range(-9, STEPS + 15):
+        for k in range(-9, STEPS):
             g, phase = divmod(k, 8)
 
             def due(lag):
@@ -343,49 +337,98 @@ def tile_fr_pb_kernel(tc, x1, x2, FE_x1, FE_x2, g1, g2, p1_w, p1_b, p2_w, p2_b, 
                 xs_to_channels(k - 5)
             if due(-1):
                 r_to_positions(k + 1)
-            late = k >= STEPS
             old = projected
             projected = []
-            for unit in waiting[: LATE if late else 1]:
-                if k > STEPS and count % 2 == 1:
-                    project(unit, "r", 3)
-                else:
-                    project(unit, "acc", 2)
-                count += 1
+            for unit in waiting[:1]:
+                project(unit, "acc", 2)
                 projected.append(unit)
             waiting = waiting[len(projected) :]
-            for at, unit in enumerate(old):
-                store(unit, at % 2 == 1 if late else unit[1] in (0, 2, 4))
+            for unit in old:
+                store(unit, unit[1] in (0, 2, 4))
             if phase == 5 and 1 <= g < GROUPS:
                 quantise(g - 1)
                 waiting += [(g - 1, m, 0, GROUP) for m in range(TILES)]
                 if g + 2 < GROUPS:
                     hold = small.tile([P, 1], F32, name="hold", tag="hold")
                     nc.vector.tensor_copy(out=hold[:], in_=live["y", g][:, 1, 0, 0:1])
-            if k in (STEPS + 1, STEPS + 5):
-                half = (k - STEPS) // 4
-                quantise_half(GROUPS - 1, half)
-                waiting += [(GROUPS - 1, m, HALF * half, HALF) for m in range(TILES)]
             if due(3) and (k - 3) % 2 == 0:
                 x_to_positions((k - 3) // 2)
             if 0 <= k < TILES // 2:
                 for m in (2 * k, 2 * k + 1):
                     w_to_channels(m)
             if k == 8:
-                b_t = psum.tile([P, 2, 4, P], BF16, name="b_t", tag="acc", bufs=2)
-                for w in range(2):
-                    for mm in range(4):
-                        nc.tensor.transpose(out=b_t[:, w, mm, :], in_=rows[2 + w][:, P * mm : P * mm + P], identity=ident_b[:])
-                for w in range(2):
-                    nc.vector.tensor_copy(out=bias[:, :, w : w + 1], in_=b_t[:, w, :, 0:1])
+                b_t = psum.tile([P, 4, P], BF16, name="b_t", tag="acc", bufs=2)
+                for mm in range(4):
+                    nc.tensor.transpose(out=b_t[:, mm, :], in_=b_rows[:, P * mm : P * mm + P], identity=ident_b[:])
+                nc.vector.tensor_copy(out=bias[:], in_=b_t[:, :, 0:2])
             if k in (-1, 0):
                 gate_first(1, k + 1)
             if 1 <= (k + 9) // 8 < GROUPS:
                 gate((k + 9) // 8, (k + 9) % 8)
-            if due(0) and k % 2 == 0 and not by_matmul(k):
-                rest(k // 2)
+                if (k + 9) % 8 == 7:
+                    rest(4 * ((k + 9) // 8))
             if phase == 6 and 0 <= g:
                 if g + 3 < GROUPS:
                     load("x", g + 3)
                 if g + 2 < GROUPS:
                     load("fe", g + 2)
+
+        last = STEPS - 1
+        banks = ["acc", "r", "acc", "r", "r"]
+
+        used = []
+
+        def emit(n):
+            for unit in waiting[:n]:
+                tag = banks[len(used) % len(banks)]
+                used.append(unit)
+                project(unit, tag, 3 if tag == "r" else 2)
+                projected.append(unit)
+                waiting.remove(unit)
+
+        def save(engines):
+            for engine in engines[: len(projected)]:
+                unit = projected[0]
+                store(unit, engine == "V")
+                projected.remove(unit)
+
+        def halves(half):
+            quantise_half(GROUPS - 1, half)
+            waiting.extend([(GROUPS - 1, m, HALF * half, HALF) for m in range(TILES)])
+
+        exp_shifted(last)
+        weigh(last)
+        scale_x(last - 3)
+        divide(last - 2)
+        scale_x(last - 2)
+        fuse(last - 5)
+        save("S")
+        xs_to_channels(last - 4)
+        x_to_positions(last // 2, "r", 3)
+        emit(2)
+        divide(last - 1)
+        divide(last)
+        scale_x(last - 1)
+        scale_x(last)
+        fuse(last - 4)
+        halves(0)
+        save("SS")
+        xs_to_channels(last - 3)
+        xs_to_channels(last - 2)
+        emit(4)
+        fuse(last - 3)
+        fuse(last - 2)
+        save("SVSV")
+        xs_to_channels(last - 1)
+        xs_to_channels(last)
+        emit(4)
+        fuse(last - 1)
+        fuse(last)
+        save("SSSS")
+        halves(1)
+        emit(4)
+        save("SVSV")
+        while waiting:
+            emit(2)
+            save("VS")
+        save("SV")

@@ -85,7 +85,10 @@ def tile_fr_pb_kernel(tc, x1, x2, FE_x1, FE_x2, g1, g2, p1_w, p1_b, p2_w, p2_b, 
             if piece == 0:
                 gate_tiles(g)
             y, x, s = live["y", g][:, 1 - i, j, :], live["x", g][:, i, j, :], sig[:, j, 4 * i + n : 4 * i + n + 1]
-            nc.gpsimd.tensor_scalar(out=y, in0=x, scalar1=s, scalar2=0.0, op0=ALU.mult, op1=ALU.add)
+            if g == 1 and i == 0:
+                nc.scalar.activation(out=y, in_=x, func=ACT.Copy, scale=s)
+            else:
+                nc.gpsimd.tensor_scalar(out=y, in0=x, scalar1=s, scalar2=0.0, op0=ALU.mult, op1=ALU.add)
             if piece == XF_AT:
                 nc.gpsimd.tensor_scalar(
                     out=live["xf", g][:], in0=live["x", g][:, :, OUTRIGHT:PACK, :], scalar1=1.0, scalar2=0.0, op0=ALU.mult, op1=ALU.add
@@ -228,6 +231,14 @@ def tile_fr_pb_kernel(tc, x1, x2, FE_x1, FE_x2, g1, g2, p1_w, p1_b, p2_w, p2_b, 
                     start=(i == 0), stop=(i == 1),
                 )
 
+        def warm_up(passes):
+            acc = psum.tile([P, GROUP], F32, name="acc", tag="acc", bufs=2)
+            for at in range(passes):
+                nc.tensor.matmul_mx(
+                    out=acc[:], lhsT=w_codes[:, 0:P].bitcast(FP8X4), lhsT_scale=w_scales[:, 0:P],
+                    rhs=w_codes[:, 0:GROUP].bitcast(FP8X4), rhs_scale=w_scales[:, 0:GROUP], start=True, stop=True,
+                )
+
         def store(unit, on_vector):
             g, m, first, width = unit
             n, half = divmod(g, 2)
@@ -255,10 +266,7 @@ def tile_fr_pb_kernel(tc, x1, x2, FE_x1, FE_x2, g1, g2, p1_w, p1_b, p2_w, p2_b, 
             if mm == 0:
                 live["wg", w] = const.tile([P, 4, 2, P, 2], F32, name="wg", tag="wg", align_bytes=64)
             src = live["wt", m][:].rearrange("p i u o -> p i o u")
-            if mm % 2 == 0:
-                nc.scalar.copy(out=live["wg", w][:, mm], in_=src)
-            else:
-                nc.vector.tensor_copy(out=live["wg", w][:, mm], in_=src)
+            nc.scalar.copy(out=live["wg", w][:, mm], in_=src)
             if mm == 3:
                 c = slice(8 * P * w, 8 * P * w + 8 * P)
                 nc.vector.quantize_mx(
@@ -335,6 +343,8 @@ def tile_fr_pb_kernel(tc, x1, x2, FE_x1, FE_x2, g1, g2, p1_w, p1_b, p2_w, p2_b, 
                     w_quantise(m)
             if due(5):
                 xs_to_channels(k - 5)
+            if TILES // 2 + 1 <= k < 14:
+                warm_up(1)
             if due(-1):
                 r_to_positions(k + 1)
             old = projected

@@ -218,10 +218,16 @@ def tile_fr_pb_kernel(tc, x1, x2, FE_x1, FE_x2, g1, g2, p1_w, p1_b, p2_w, p2_b, 
                     in_=live["re", g][:, i, c, :].rearrange("p c j -> p (c j)"),
                 )
 
-        def project(unit, tag, bufs):
+        def project(unit, tag, bufs, extra=False):
             g, m, first, width = unit
             acc = psum.tile([P, GROUP], F32, name="acc", tag=tag, bufs=bufs)
             live["acc", unit] = acc
+            if extra:
+                nc.tensor.matmul_mx(
+                    out=acc[:, 0:width], lhsT=w_codes[:, 0:P].bitcast(FP8X4), lhsT_scale=w_scales[:, 0:P],
+                    rhs=live["codes", g][:, first : first + width].bitcast(FP8X4), rhs_scale=live["scales", g][:, first : first + width],
+                    start=True, stop=True,
+                )
             for i in range(2):
                 wc = slice((2 * m + i) * P, (2 * m + i) * P + P)
                 rc = slice(GROUP * i + first, GROUP * i + first + width)
@@ -350,7 +356,7 @@ def tile_fr_pb_kernel(tc, x1, x2, FE_x1, FE_x2, g1, g2, p1_w, p1_b, p2_w, p2_b, 
             old = projected
             projected = []
             for unit in waiting[:1]:
-                project(unit, "acc", 2)
+                project(unit, "acc", 2, due(5) and not by_matmul(k - 5))
                 projected.append(unit)
             waiting = waiting[len(projected) :]
             for unit in old:
@@ -373,7 +379,10 @@ def tile_fr_pb_kernel(tc, x1, x2, FE_x1, FE_x2, g1, g2, p1_w, p1_b, p2_w, p2_b, 
                 nc.vector.tensor_copy(out=bias[:], in_=b_t[:, :, 0:2])
             if k in (-1, 0):
                 gate_first(1, k + 1)
-            if 1 <= (k + 9) // 8 < GROUPS:
+            if k == -1:
+                for piece in range(PACK):
+                    gate(1, piece)
+            if 3 <= k and (k + 9) // 8 < GROUPS:
                 gate((k + 9) // 8, (k + 9) % 8)
                 if (k + 9) % 8 == 7:
                     rest(4 * ((k + 9) // 8))

from contextlib import ExitStack

import concourse.mybir as mybir
from concourse.masks import make_identity

F32 = mybir.dt.float32
BF16 = mybir.dt.bfloat16
U32 = mybir.dt.uint32
U8 = mybir.dt.uint8
FP8X4 = mybir.dt.float8_e4m3fn_x4
ALU = mybir.AluOpType
ACT = mybir.ActivationFunctionType
AX = mybir.AxisListType

FLOPS = 2 * 1024 * 1024 * 4096

P = 128
PACK = 4
GROUP = 512
HALF = 256
STEPS = 64
GROUPS = 8
TILES = 8
XF_AT = 3
OUTRIGHT = 2


def by_matmul(h):
    return h < 8 or h % 8 >= 2


def outright(g, j):
    return g == 0 or j < OUTRIGHT


def tile_fr_pb_kernel(tc, x1, x2, FE_x1, FE_x2, g1, g2, p1_w, p1_b, p2_w, p2_b, out_0, out_1):
    nc = tc.nc
    x_hbm = [a.rearrange("n (p j) h w -> n p j (h w)", j=PACK) for a in (x1, x2)]
    fe_hbm = [a.rearrange("n (p j) h w -> n p j (h w)", j=PACK) for a in (FE_x1, FE_x2)]
    w_hbm = [a.rearrange("(m p) k -> p m k", p=P) for a in (p1_w, p2_w)]
    out_hbm = [a.rearrange("n (m p) h w -> n m p (h w)", p=P) for a in (out_0, out_1)]

    with ExitStack() as ctx:
        const = ctx.enter_context(tc.tile_pool(name="const", bufs=1))
        groups = ctx.enter_context(tc.tile_pool(name="groups", bufs=2))
        steps = ctx.enter_context(tc.tile_pool(name="steps", bufs=3))
        small = ctx.enter_context(tc.tile_pool(name="small", bufs=4))
        psum = ctx.enter_context(tc.psum_pool(name="psum", bufs=1))
        ctx.enter_context(tc.manual_schedule())

        live = {}

        def place(h):
            block, i = divmod(h, 2)
            g, b = divmod(block, 4)
            return block, i, g, slice(P * b, P * b + P)


        def load(kind, g):
            n, half = divmod(g, 2)
            cols = slice(GROUP * half, GROUP * half + GROUP)
            hbm, bufs = {"x": (x_hbm, 4), "fe": (fe_hbm, 3)}[kind]
            t = groups.tile([P, 2, PACK, GROUP], BF16, name=kind, tag=kind, bufs=bufs)
            live[kind, g] = t
            for i in range(2):
                nc.sync.dma_start(out=t[:, i if kind == "x" else 1 - i], in_=hbm[i][n][:, :, cols])

        def gate_tiles(g):
            live["y", g] = groups.tile([P, 2, PACK, GROUP], F32, name="y", tag="y")
            if g > 0:
                live["xf", g] = groups.tile([P, 2, PACK - OUTRIGHT, GROUP], F32, name="xf", tag="xf")

        def gate_first(half, i):
            if half == 0 and i == 0:
                gate_tiles(0)
            c = slice(HALF * half, HALF * half + HALF)
            for j in reversed(range(PACK)):
                y, x, s = live["y", 0][:, 1 - i, j, c], live["x", 0][:, i, j, c], sig[:, j, 4 * i : 4 * i + 1]
                xj = live["x", 0][:, 1 - i, j, c]
                nc.vector.scalar_tensor_tensor(out=y, in0=x, scalar=s, in1=xj, op0=ALU.mult, op1=ALU.add)

        def gate(g, piece):
            n = g // 2
            i, j = divmod(piece, PACK)
            if piece == 0:
                gate_tiles(g)
            y, x, s = live["y", g][:, 1 - i, j, :], live["x", g][:, i, j, :], sig[:, j, 4 * i + n : 4 * i + n + 1]
            if g == 1 and i == 0:
                nc.scalar.activation(out=y, in_=x, func=ACT.Copy, scale=s)
            else:
                nc.gpsimd.tensor_scalar(out=y, in0=x, scalar1=s, scalar2=0.0, op0=ALU.mult, op1=ALU.add)
            if piece == XF_AT:
                nc.gpsimd.tensor_scalar(
                    out=live["xf", g][:], in0=live["x", g][:, :, OUTRIGHT:PACK, :], scalar1=1.0, scalar2=0.0, op0=ALU.mult, op1=ALU.add
                )
            if j == PACK - 1 and (g == 1 or i == 1):
                o = slice(1 - i, 2 - i) if g == 1 else slice(0, 2)
                yo = live["y", g][:, o, 0:OUTRIGHT, :]
                nc.gpsimd.tensor_tensor(out=yo, in0=yo, in1=live["x", g][:, o, 0:OUTRIGHT, :], op=ALU.add)

        def rest(block):
            g, b = divmod(block, 4)
            cols = slice(P * b, P * b + P)
            live["u", block] = steps.tile([P, 2, PACK, P], F32, name="u", tag="u", bufs=2)
            nc.gpsimd.tensor_tensor(out=live["u", block][:], in0=live["x", g][:, :, :, cols], in1=live["fe", g][:, :, :, cols], op=ALU.add)


        def r_to_positions(h):
            block, i, g, cols = place(h)
            r = psum.tile([P, PACK * P], F32, name="r", tag="r", bufs=3)
            live["r", h] = r
            parts = [(live["y", g][:, 1 - i, j, cols], j) for j in range(PACK)]
            parts += [(live["xf", g][:, 1 - i, j - OUTRIGHT, cols], j) for j in range(PACK) if not outright(g, j)]
            for at, (part, j) in enumerate(parts):
                nc.tensor.matmul(r[:, j * P : j * P + P], lhsT=part, rhs=ident_f[:], is_transpose=True, start=(at == 0), stop=(at == len(parts) - 1))

        def exp_r(h):
            a = steps.tile([P, PACK * P], F32, name="a", tag="a")
            live["a", h] = a
            nc.scalar.activation(out=a[:], in_=live["r", h][:], func=ACT.Exp)

        def neg_max(h):
            m = small.tile([P, 1], F32, name="negmax", tag="negmax")
            live["negmax", h] = m
            nc.vector.tensor_reduce(out=m[:], in_=live["a", h][:], axis=AX.X, op=ALU.max, negate=True)

        def exp_shifted(h):
            block, i, g, cols = place(h)
            if i == 0:
                live["sum_e", block] = small.tile([P, 2], F32, name="sum_e", tag="sum_e")
            e = steps.tile([P, PACK * P], F32, name="e", tag="e")
            live["e", h] = e
            nc.scalar.activation(
                out=e[:], in_=live["a", h][:], func=ACT.Exp, bias=live["negmax", h][:], scale=1.0, accum_out=live["sum_e", block][:, i : i + 1]
            )

        def weigh(h):
            block, i, g, cols = place(h)
            if i == 0:
                live["sum_er", block] = small.tile([P, 2], F32, name="sum_er", tag="sum_er")
            e = live["e", h]
            nc.vector.scalar_tensor_tensor(
                out=e[:], in0=e[:], scalar=1.0, in1=live["r", h][:], op0=ALU.mult, op1=ALU.mult, accum_out=live["sum_er", block][:, i : i + 1]
            )
            if i == 1:
                inv = small.tile([P, 2], F32, name="inv", tag="inv")
                live["inv", block] = inv
                nc.vector.reciprocal(out=inv[:], in_=live["sum_e", block][:])

        def divide(h):
            block, i, g, cols = place(h)
            if i == 0:
                live["s", block] = small.tile([P, 2], F32, name="s", tag="s")
            nc.scalar.activation(
                out=live["s", block][:, i : i + 1], in_=live["sum_er", block][:, i : i + 1], func=ACT.Copy, scale=live["inv", block][:, i : i + 1]
            )


        def x_to_positions(block, tag="xt", bufs=1):
            g, b = divmod(block, 4)
            cols = slice(P * b, P * b + P)
            xt = psum.tile([P, 2, PACK * P], BF16, name="xt", tag=tag, bufs=bufs)
            live["xt", block] = xt
            for i in range(2):
                for j in range(PACK):
                    nc.tensor.transpose(out=xt[:, i, P * j : P * j + P], in_=live["x", g][:, i, j, cols], identity=ident_b[:])

        def scale_x(h):
            block, i, g, cols = place(h)
            t = steps.tile([P, PACK * P], F32, name="xs", tag="xs", bufs=4)
            live["xs", h] = t
            nc.scalar.activation(out=t[:], in_=live["xt", block][:, i, :], func=ACT.Copy, scale=live["s", block][:, i : i + 1])

        def xs_to_channels(h):
            block, i, g, cols = place(h)
            z = psum.tile([P, PACK, P], F32, name="z", tag="z", bufs=2)
            live["z", h] = z
            plain = by_matmul(h)
            for j in range(PACK):
                nc.tensor.matmul(
                    z[:, j, :], lhsT=live["xs", h][:, P * j : P * j + P], rhs=ident_f[:], is_transpose=True,
                    start=(j == 0), stop=(j == PACK - 1 and not plain),
                )
            if plain:
                nc.tensor.matmul(z[:], lhsT=ident_b[:], rhs=live["x", g][:, 1 - i, :, cols], start=False, stop=True)

        def fuse(h):
            block, i, g, cols = place(h)
            if h % 8 == 0:
                live["re", g] = groups.tile([P, 2, GROUP, PACK], BF16, name="re", tag="re", align_bytes=64)
            add = live["fe", g][:, 1 - i, :, cols] if by_matmul(h) else live["u", block][:, 1 - i]
            nc.vector.tensor_tensor(
                out=live["re", g][:, i, cols, :].rearrange("p (c f) j -> p c j f", f=4),
                in0=live["z", h][:].rearrange("p j (c f) -> p c j f", f=4),
                in1=add.rearrange("p j (c f) -> p c j f", f=4),
                op=ALU.add,
            )


        def mx_tiles(g):
            live["codes", g] = groups.tile([P, 2 * GROUP], U32, name="codes", tag="codes", align_bytes=64)
            live["scales", g] = groups.tile([P, 2 * GROUP], U8, name="scales", tag="scales", align_bytes=64)

        def quantise(g):
            mx_tiles(g)
            nc.vector.quantize_mx(
                out=live["codes", g][:].bitcast(FP8X4), scales=live["scales", g][:], in_=live["re", g][:].rearrange("p i c j -> p (i c j)")
            )

        def quantise_half(g, half):
            if half == 0:
                mx_tiles(g)
            for i in range(2):
                c = slice(HALF * half, HALF * half + HALF)
                w = slice(GROUP * i + HALF * half, GROUP * i + HALF * half + HALF)
                nc.vector.quantize_mx(
                    out=live["codes", g][:, w].bitcast(FP8X4), scales=live["scales", g][:, w],
                    in_=live["re", g][:, i, c, :].rearrange("p c j -> p (c j)"),
                )

        def project(unit, tag, bufs, extra=False):
            g, m, first, width = unit
            acc = psum.tile([P, GROUP], F32, name="acc", tag=tag, bufs=bufs)
            live["acc", unit] = acc
            if extra:
                nc.tensor.matmul_mx(
                    out=acc[:, 0:width], lhsT=w_codes[:, 0:P].bitcast(FP8X4), lhsT_scale=w_scales[:, 0:P],
                    rhs=live["codes", g][:, first : first + width].bitcast(FP8X4), rhs_scale=live["scales", g][:, first : first + width],
                    start=True, stop=True,
                )
            for i in range(2):
                wc = slice((2 * m + i) * P, (2 * m + i) * P + P)
                rc = slice(GROUP * i + first, GROUP * i + first + width)
                nc.tensor.matmul_mx(
                    out=acc[:, 0:width], lhsT=w_codes[:, wc].bitcast(FP8X4), lhsT_scale=w_scales[:, wc],
                    rhs=live["codes", g][:, rc].bitcast(FP8X4), rhs_scale=live["scales", g][:, rc],
                    start=(i == 0), stop=(i == 1),
                )

        def warm_up(passes):
            acc = psum.tile([P, GROUP], F32, name="acc", tag="acc", bufs=2)
            for at in range(passes):
                nc.tensor.matmul_mx(
                    out=acc[:], lhsT=w_codes[:, 0:P].bitcast(FP8X4), lhsT_scale=w_scales[:, 0:P],
                    rhs=w_codes[:, 0:GROUP].bitcast(FP8X4), rhs_scale=w_scales[:, 0:GROUP], start=True, stop=True,
                )

        def store(unit, on_vector):
            g, m, first, width = unit
            n, half = divmod(g, 2)
            w, mm = divmod(m, 4)
            o = steps.tile([P, GROUP], F32, name="o", tag="o", bufs=12)
            b = bias[:, mm, w : w + 1]
            acc = live["acc", unit][:, 0:width]
            if on_vector:
                nc.vector.tensor_scalar(out=o[:, 0:width], in0=acc, scalar1=b, scalar2=None, op0=ALU.add)
            else:
                nc.scalar.activation(out=o[:, 0:width], in_=acc, func=ACT.Identity, bias=b, scale=1.0)
            nc.sync.dma_start(out=out_hbm[w][n, mm][:, GROUP * half + first : GROUP * half + first + width], in_=o[:, 0:width])

        def w_to_channels(m):
            w, mm = divmod(m, 4)
            wt = psum.tile([P, 2, 2, P], F32, name="wt", tag="acc", bufs=2)
            live["wt", m] = wt
            words = w_raw[w][:, mm, :].bitcast(F32).rearrange("o (i p u) -> o i u p", i=2, u=2)
            for i in range(2):
                for u in range(2):
                    nc.tensor.transpose(out=wt[:, i, u, :], in_=words[:, i, u, :], identity=ident_f[:])

        def w_quantise(m):
            w, mm = divmod(m, 4)
            if mm == 0:
                live["wg", w] = const.tile([P, 4, 2, P, 2], F32, name="wg", tag="wg", align_bytes=64)
            src = live["wt", m][:].rearrange("p i u o -> p i o u")
            nc.scalar.copy(out=live["wg", w][:, mm], in_=src)
            if mm == 3:
                c = slice(8 * P * w, 8 * P * w + 8 * P)
                nc.vector.quantize_mx(
                    out=w_codes[:, c].bitcast(FP8X4), scales=w_scales[:, c],
                    in_=live["wg", w][:].rearrange("p m i o u -> p (m i o u)").bitcast(BF16),
                )


        g_rows = const.tile([P, PACK * P], BF16, name="g_rows")
        nc.vector.memset(g_rows[:], 0.0)
        for i, src in enumerate((g1, g2)):
            nc.sync.dma_start(out=g_rows[4 * i : 4 * i + 4, :], in_=src)
        warm = const.tile([P, 1], F32, name="warm")
        nc.vector.memset(warm[:], 0.0)
        nc.scalar.activation(out=warm[:], in_=warm[:], func=ACT.Exp)
        load("x", 0)
        load("x", 1)
        w_raw = []
        for w in range(2):
            t = const.tile([P, 4, 1024], BF16, name="w_raw%d" % w)
            nc.sync.dma_start(out=t[:], in_=w_hbm[w])
            w_raw.append(t)
        load("fe", 0)
        b_rows = const.tile([P, PACK * P], BF16, name="b_rows")
        nc.vector.memset(b_rows[:], 0.0)
        for w, src in enumerate((p1_b, p2_b)):
            nc.sync.dma_start(out=b_rows[w : w + 1, :], in_=src.rearrange("(o c) -> o c", o=1))
        ident_b = const.tile([P, P], BF16, name="ident_b")
        make_identity(nc, ident_b[:])
        ident_f = const.tile([P, P], F32, name="ident_f")
        make_identity(nc, ident_f[:])
        load("fe", 1)
        load("x", 2)
        w_codes = const.tile([P, 2 * TILES * P], U32, name="w_codes", align_bytes=64)
        w_scales = const.tile([P, 2 * TILES * P], U8, name="w_scales", align_bytes=64)

        g_t = psum.tile([P, PACK, P], BF16, name="g_t", tag="xt", bufs=1)
        by_j = const.tile([P, PACK, P], BF16, name="by_j")
        nc.vector.tensor_copy(out=by_j[:], in_=g_rows[:].rearrange("r (p j) -> r j p", j=PACK))
        for j in range(PACK):
            nc.tensor.transpose(out=g_t[:, j, :], in_=by_j[:, j, :], identity=ident_b[:])
        sig = const.tile([P, PACK, 8], F32, name="sig")
        nc.scalar.activation(out=sig[:], in_=g_t[:, :, 0:8], func=ACT.Exp, scale=-1.0)
        nc.vector.tensor_scalar(out=sig[:], in0=sig[:], scalar1=1.0, scalar2=None, op0=ALU.add)
        nc.vector.reciprocal(out=sig[:], in_=sig[:])
        bias = const.tile([P, 4, 2], F32, name="bias")

        waiting = []
        projected = []
        for k in range(-9, STEPS):
            g, phase = divmod(k, 8)

            def due(lag):
                return 0 <= k - lag < STEPS

            if k in (-2, -1):
                gate_first(0, k + 2)
            if due(0):
                exp_r(k)
            if due(1):
                exp_shifted(k - 1)
            if due(6):
                fuse(k - 6)
            if due(0):
                neg_max(k)
            if due(1):
                weigh(k - 1)
            if due(3):
                divide(k - 3)
            if due(4):
                scale_x(k - 4)
            if 1 <= k < 1 + TILES // 2:
                for m in (2 * k - 2, 2 * k - 1):
                    w_quantise(m)
            if due(5):
                xs_to_channels(k - 5)
            if TILES // 2 + 1 <= k < 14:
                warm_up(1)
            if due(-1):
                r_to_positions(k + 1)
            old = projected
            projected = []
            for unit in waiting[:1]:
                project(unit, "acc", 2, due(5) and not by_matmul(k - 5))
                projected.append(unit)
            waiting = waiting[len(projected) :]
            for unit in old:
                store(unit, unit[1] in (0, 2, 4))
            if phase == 5 and 1 <= g < GROUPS:
                quantise(g - 1)
                waiting += [(g - 1, m, 0, GROUP) for m in range(TILES)]
                if g + 2 < GROUPS:
                    hold = small.tile([P, 1], F32, name="hold", tag="hold")
                    nc.vector.tensor_copy(out=hold[:], in_=live["y", g][:, 1, 0, 0:1])
            if due(3) and (k - 3) % 2 == 0:
                x_to_positions((k - 3) // 2)
            if 0 <= k < TILES // 2:
                for m in (2 * k, 2 * k + 1):
                    w_to_channels(m)
            if k == 8:
                b_t = psum.tile([P, 4, P], BF16, name="b_t", tag="acc", bufs=2)
                for mm in range(4):
                    nc.tensor.transpose(out=b_t[:, mm, :], in_=b_rows[:, P * mm : P * mm + P], identity=ident_b[:])
                nc.vector.tensor_copy(out=bias[:], in_=b_t[:, :, 0:2])
            if k in (-1, 0):
                gate_first(1, k + 1)
            if k == -1:
                for piece in range(PACK):
                    gate(1, piece)
            if 3 <= k and (k + 9) // 8 < GROUPS:
                gate((k + 9) // 8, (k + 9) % 8)
                if (k + 9) % 8 == 7:
                    rest(4 * ((k + 9) // 8))
            if phase == 6 and 0 <= g:
                if g + 3 < GROUPS:
                    load("x", g + 3)
                if g + 2 < GROUPS:
                    load("fe", g + 2)

        last = STEPS - 1
        banks = ["acc", "r", "acc", "r", "r"]

        used = []

        def emit(n):
            for unit in waiting[:n]:
                tag = banks[len(used) % len(banks)]
                used.append(unit)
                project(unit, tag, 3 if tag == "r" else 2)
                projected.append(unit)
                waiting.remove(unit)

        def save(engines):
            for engine in engines[: len(projected)]:
                unit = projected[0]
                store(unit, engine == "V")
                projected.remove(unit)

        def halves(half):
            quantise_half(GROUPS - 1, half)
            waiting.extend([(GROUPS - 1, m, HALF * half, HALF) for m in range(TILES)])

        exp_shifted(last)
        weigh(last)
        scale_x(last - 3)
        divide(last - 2)
        scale_x(last - 2)
        fuse(last - 5)
        save("S")
        xs_to_channels(last - 4)
        x_to_positions(last // 2, "r", 3)
        emit(2)
        divide(last - 1)
        divide(last)
        scale_x(last - 1)
        scale_x(last)
        fuse(last - 4)
        halves(0)
        save("SS")
        xs_to_channels(last - 3)
        xs_to_channels(last - 2)
        emit(4)
        fuse(last - 3)
        fuse(last - 2)
        save("SVSV")
        xs_to_channels(last - 1)
        xs_to_channels(last)
        emit(4)
        fuse(last - 1)
        fuse(last)
        save("SSSS")
        halves(1)
        emit(4)
        save("SVSV")
        while waiting:
            emit(2)
            save("VS")
        save("SV")
